import numpy as np
import ml_dtypes


def mxq(x, axis, fmt="e4m3"):
    dtype, down = {"e4m3": (ml_dtypes.float8_e4m3fn, 7), "e5m2": (ml_dtypes.float8_e5m2, 14)}[fmt]
    v = np.moveaxis(np.asarray(x, np.float32).astype(ml_dtypes.bfloat16).astype(np.float64), axis, -1)
    blocks = v.reshape(v.shape[:-1] + (-1, 32))
    amax = np.abs(blocks).max(-1, keepdims=True)
    byte = np.maximum(np.where(amax > 0, np.frexp(amax)[1] - 1 + 127, 0) - down, 1)
    scale = np.exp2(byte - 127.0)
    codes = (blocks / scale).astype(np.float32).astype(dtype).astype(np.float64)
    return np.moveaxis((codes * scale).reshape(v.shape), -1, axis)


WIDE = False


def mx_kscale(k):
    if not WIDE:
        return np.ones(k)
    levels = np.array([10, -10, 5, -5, 0])
    a = np.random.permutation(np.resize(levels, k // 512 * 4)).reshape(k // 512, 4)
    idx = np.arange(k)
    return np.exp2(a[idx // 512, idx % 128 // 32])


BF16 = ml_dtypes.bfloat16


def bf(x):
    return np.asarray(x, np.float32).astype(BF16)


def f64(x):
    return np.asarray(x).astype(np.float64)


B, D, A = 1024, 1024, 1024


def setup_inputs():
    s = mx_kscale(D)
    return {
        "x": bf(np.random.standard_normal((B, D)) * s),
        "saved_x": bf(np.random.standard_normal((B, D)) * s),
        "saved_a": bf(np.random.standard_normal((B, A))),
        "saved_b": bf(0.5 + np.random.random((B, A))),
        "saved_p": bf(np.random.standard_normal((B, A))),
        "time_decay": bf(np.random.standard_normal(A)),
        "time_first": bf(np.random.standard_normal(A)),
        "k_mixed": bf(np.random.random(D)),
        "v_mixed": bf(np.random.random(D)),
        "key_weight": bf(np.random.standard_normal((D, A)) / np.sqrt(D) / s[:, None]),
        "value_weight": bf(np.random.standard_normal((D, A)) / np.sqrt(D) / s[:, None]),
    }


def reference(x, saved_x, saved_a, saved_b, saved_p, time_decay, time_first, k_mixed, v_mixed, key_weight, value_weight):
    x, saved_x = f64(x), f64(saved_x)
    saved_a, saved_b, saved_p = f64(saved_a), f64(saved_b), f64(saved_p)
    time_decay, time_first = f64(time_decay), f64(time_first)
    k_mixed, v_mixed = f64(k_mixed), f64(v_mixed)
    xk = x * k_mixed + saved_x * (1.0 - k_mixed)
    xv = x * v_mixed + saved_x * (1.0 - v_mixed)
    k = mxq(xk, 1, "e4m3") @ mxq(f64(key_weight), 0, "e4m3")
    v = mxq(xv, 1, "e4m3") @ mxq(f64(value_weight), 0, "e4m3")
    w = k + time_first
    p = np.maximum(saved_p, w)
    e1 = np.exp(saved_p - p)
    e2 = np.exp(w - p)
    wkv = (e1 * saved_a + e2 * v) / (e1 * saved_b + e2)
    w2 = saved_p + time_decay
    p2 = np.maximum(w2, k)
    f1 = np.exp(w2 - p2)
    f2 = np.exp(k - p2)
    aa = f1 * saved_a + f2 * v
    bb = f1 * saved_b + f2
    return wkv, aa, bb, p2

@@ -1,0 +1,256 @@
+from contextlib import ExitStack
+
+import concourse.mybir as mybir
+from concourse.masks import make_identity
+
+F32 = mybir.dt.float32
+BF16 = mybir.dt.bfloat16
+U32 = mybir.dt.uint32
+U8 = mybir.dt.uint8
+FP8X4 = mybir.dt.float8_e4m3fn_x4
+ALU = mybir.AluOpType
+FUNC = mybir.ActivationFunctionType
+
+P = 128
+PACK = 4
+K_PASS = P * PACK
+ROWS = 1024
+DEPTH = 1024
+WIDTH = 1024
+PASSES = DEPTH // K_PASS
+CHUNKS = DEPTH // P
+ROW_TILES = ROWS // P
+N_TILE = 512
+COL_TILES = WIDTH // N_TILE
+
+FLOPS = 2 * 2 * ROWS * DEPTH * WIDTH
+
+
+def interleave(copy, grouped, planes):
+    copy(
+        out=grouped.rearrange("p (c i) t -> p c t i", i=4),
+        in_=planes.rearrange("p t (c i) -> p c t i", i=4),
+    )
+
+
+def quantise(nc, grouped, codes, scales):
+    nc.vector.quantize_mx(
+        out=codes.bitcast(FP8X4),
+        scales=scales,
+        in_=grouped.rearrange("p c t -> p (c t)"),
+    )
+
+
+def blend(nc, work, old_raw, new_raw, a_cols, b_cols, v_ps, top, bottom):
+    new_v = work.tile([P, N_TILE], F32)
+    nc.vector.scalar_tensor_tensor(
+        out=top, in0=old_raw, scalar=1.0, in1=a_cols, op0=ALU.min, op1=ALU.mult
+    )
+    nc.vector.scalar_tensor_tensor(
+        out=new_v[:], in0=new_raw, scalar=1.0, in1=v_ps, op0=ALU.min, op1=ALU.mult
+    )
+    nc.vector.scalar_tensor_tensor(
+        out=bottom, in0=old_raw, scalar=1.0, in1=b_cols, op0=ALU.min, op1=ALU.mult
+    )
+    nc.vector.tensor_tensor(out=top, in0=top, in1=new_v[:], op=ALU.add)
+    nc.vector.scalar_tensor_tensor(
+        out=bottom, in0=new_raw, scalar=1.0, in1=bottom, op0=ALU.min, op1=ALU.add
+    )
+
+
+def tile_rwkv_attention_pa_kernel(
+    tc,
+    x,
+    saved_x,
+    saved_a,
+    saved_b,
+    saved_p,
+    time_decay,
+    time_first,
+    k_mixed,
+    v_mixed,
+    key_weight,
+    value_weight,
+    out_0,
+    out_1,
+    out_2,
+    out_3,
+):
+    nc = tc.nc
+    with ExitStack() as pools:
+        keep = pools.enter_context(tc.tile_pool(name="keep", bufs=1))
+        state = pools.enter_context(tc.tile_pool(name="state", bufs=3))
+        turned = pools.enter_context(tc.psum_pool(name="turned", bufs=2))
+        products = pools.enter_context(tc.psum_pool(name="products", bufs=2))
+
+        xk_codes = keep.tile([P, PASSES, ROWS], U32, align_bytes=64)
+        xv_codes = keep.tile([P, PASSES, ROWS], U32, align_bytes=64)
+        wk_codes = keep.tile([P, PASSES, WIDTH], U32, align_bytes=64)
+        wv_codes = keep.tile([P, PASSES, WIDTH], U32, align_bytes=64)
+        xk_scales = keep.tile([P, PASSES, ROWS], U8, align_bytes=64)
+        xv_scales = keep.tile([P, PASSES, ROWS], U8, align_bytes=64)
+        wk_scales = keep.tile([P, PASSES, WIDTH], U8, align_bytes=64)
+        wv_scales = keep.tile([P, PASSES, WIDTH], U8, align_bytes=64)
+
+        decay = keep.tile([P, WIDTH], BF16)
+        first = keep.tile([P, WIDTH], BF16)
+
+        ident = keep.tile([P, P], BF16)
+        make_identity(nc, ident[:])
+
+        mix_rows = keep.tile([P, P], BF16)
+        nc.vector.memset(mix_rows[:], 0.0)
+        nc.sync.dma_start(out=mix_rows[0:CHUNKS, :], in_=k_mixed.rearrange("(c p) -> c p", p=P))
+        nc.sync.dma_start(
+            out=mix_rows[CHUNKS : 2 * CHUNKS, :], in_=v_mixed.rearrange("(c p) -> c p", p=P)
+        )
+        mix_turned = turned.tile([P, P], BF16, tag="x_turned")
+        nc.tensor.transpose(mix_turned[:], mix_rows[:], ident[:])
+        mix = keep.tile([P, 2 * CHUNKS], F32)
+        nc.vector.tensor_copy(out=mix[:], in_=mix_turned[:, 0 : 2 * CHUNKS])
+        one_minus_mix = keep.tile([P, 2 * CHUNKS], F32)
+        nc.vector.tensor_scalar(
+            out=one_minus_mix[:], in0=mix[:], scalar1=-1.0, scalar2=1.0, op0=ALU.mult, op1=ALU.add
+        )
+
+        with ExitStack() as operand_pools:
+            whole = operand_pools.enter_context(tc.tile_pool(name="whole", bufs=1))
+            raw = operand_pools.enter_context(tc.tile_pool(name="raw", bufs=4))
+            stage = operand_pools.enter_context(tc.tile_pool(name="stage", bufs=2))
+            group = operand_pools.enter_context(tc.tile_pool(name="group", bufs=3))
+
+            x_rows = whole.tile([P, ROW_TILES, DEPTH], BF16)
+            s_rows = whole.tile([P, ROW_TILES, DEPTH], BF16)
+            x_view = x.rearrange("(r p) d -> p r d", p=P)
+            s_view = saved_x.rearrange("(r p) d -> p r d", p=P)
+            wk_view = key_weight.rearrange("(g t p) a -> g p t a", t=PACK, p=P)
+            wv_view = value_weight.rearrange("(g t p) a -> g p t a", t=PACK, p=P)
+
+            for g in range(PASSES):
+                depth = slice(g * K_PASS, (g + 1) * K_PASS)
+
+                for view, codes, scales in (
+                    (wk_view, wk_codes, wk_scales),
+                    (wv_view, wv_codes, wv_scales),
+                ):
+                    w_planes = raw.tile([P, PACK, WIDTH], BF16)
+                    nc.sync.dma_start(out=w_planes[:], in_=view[g])
+                    w_grouped = group.tile([P, WIDTH, PACK], BF16, tag="grouped", align_bytes=64)
+                    interleave(nc.vector.tensor_copy, w_grouped[:], w_planes[:])
+                    quantise(nc, w_grouped[:], codes[:, g, :], scales[:, g, :])
+
+                nc.sync.dma_start(out=x_rows[:, :, depth], in_=x_view[:, :, depth])
+                nc.sync.dma_start(out=s_rows[:, :, depth], in_=s_view[:, :, depth])
+                k_planes = stage.tile([P, PACK, ROWS], BF16)
+                v_planes = stage.tile([P, PACK, ROWS], BF16)
+                for t in range(PACK):
+                    c = g * PACK + t
+                    x_turned = turned.tile([P, ROWS], BF16)
+                    s_turned = turned.tile([P, ROWS], BF16)
+                    for r in range(ROW_TILES):
+                        nc.tensor.transpose(
+                            x_turned[:, r * P : (r + 1) * P],
+                            x_rows[:, r, c * P : (c + 1) * P],
+                            ident[:],
+                        )
+                    for r in range(ROW_TILES):
+                        nc.tensor.transpose(
+                            s_turned[:, r * P : (r + 1) * P],
+                            s_rows[:, r, c * P : (c + 1) * P],
+                            ident[:],
+                        )
+                    for planes, col in ((k_planes, c), (v_planes, CHUNKS + c)):
+                        old_part = stage.tile([P, ROWS], F32)
+                        nc.scalar.activation(
+                            out=old_part[:],
+                            in_=s_turned[:],
+                            func=FUNC.Copy,
+                            scale=one_minus_mix[:, col : col + 1],
+                        )
+                        nc.vector.scalar_tensor_tensor(
+                            out=planes[:, t, :],
+                            in0=x_turned[:],
+                            scalar=mix[:, col : col + 1],
+                            in1=old_part[:],
+                            op0=ALU.mult,
+                            op1=ALU.add,
+                        )
+                for planes, codes, scales in (
+                    (k_planes, xk_codes, xk_scales),
+                    (v_planes, xv_codes, xv_scales),
+                ):
+                    x_grouped = group.tile([P, ROWS, PACK], BF16, tag="grouped", align_bytes=64)
+                    interleave(nc.scalar.copy, x_grouped[:], planes[:])
+                    quantise(nc, x_grouped[:], codes[:, g, :], scales[:, g, :])
+
+        nc.sync.dma_start(out=decay[:], in_=time_decay.partition_broadcast(P))
+        nc.sync.dma_start(out=first[:], in_=time_first.partition_broadcast(P))
+
+        work = pools.enter_context(tc.tile_pool(name="work", bufs=3))
+        for r in range(ROW_TILES):
+            rows = slice(r * P, (r + 1) * P)
+            a_rows = state.tile([P, WIDTH], BF16)
+            b_rows = state.tile([P, WIDTH], BF16)
+            p_rows = state.tile([P, WIDTH], BF16)
+            nc.sync.dma_start(out=p_rows[:], in_=saved_p[rows, :])
+            nc.sync.dma_start(out=a_rows[:], in_=saved_a[rows, :])
+            nc.sync.dma_start(out=b_rows[:], in_=saved_b[rows, :])
+            for h in range(COL_TILES):
+                cols = slice(h * N_TILE, (h + 1) * N_TILE)
+
+                k_ps = products.tile([P, N_TILE], F32)
+                v_ps = products.tile([P, N_TILE], F32)
+                for acc, x_codes, x_scales, w_codes, w_scales in (
+                    (k_ps, xk_codes, xk_scales, wk_codes, wk_scales),
+                    (v_ps, xv_codes, xv_scales, wv_codes, wv_scales),
+                ):
+                    for g in range(PASSES):
+                        nc.tensor.matmul_mx(
+                            out=acc[:],
+                            lhsT=x_codes[:, g, rows].bitcast(FP8X4),
+                            lhsT_scale=x_scales[:, g, rows],
+                            rhs=w_codes[:, g, cols].bitcast(FP8X4),
+                            rhs_scale=w_scales[:, g, cols],
+                            start=(g == 0),
+                            stop=(g == PASSES - 1),
+                        )
+
+                lead = work.tile([P, N_TILE], F32)
+                nc.vector.tensor_tensor(out=lead[:], in0=k_ps[:], in1=p_rows[:, cols], op=ALU.subtract)
+                behind = work.tile([P, N_TILE], F32)
+                nc.vector.tensor_tensor(out=behind[:], in0=decay[:, cols], in1=lead[:], op=ALU.subtract)
+                ahead = work.tile([P, N_TILE], F32)
+                nc.vector.tensor_tensor(out=ahead[:], in0=lead[:], in1=first[:, cols], op=ALU.add)
+
+                p2 = work.tile([P, N_TILE], F32)
+                nc.vector.scalar_tensor_tensor(
+                    out=p2[:], in0=behind[:], scalar=0.0, in1=k_ps[:], op0=ALU.max, op1=ALU.add
+                )
+                nc.sync.dma_start(out=out_3[rows, cols], in_=p2[:])
+
+                f1_raw = work.tile([P, N_TILE], F32)
+                f2_raw = work.tile([P, N_TILE], F32)
+                e1_raw = work.tile([P, N_TILE], F32)
+                e2_raw = work.tile([P, N_TILE], F32)
+                nc.scalar.activation(out=f1_raw[:], in_=behind[:], func=FUNC.Exp)
+                nc.scalar.activation(out=f2_raw[:], in_=behind[:], func=FUNC.Exp, scale=-1.0)
+                nc.scalar.activation(out=e1_raw[:], in_=ahead[:], func=FUNC.Exp, scale=-1.0)
+                nc.scalar.activation(out=e2_raw[:], in_=ahead[:], func=FUNC.Exp)
+
+                aa = work.tile([P, N_TILE], F32)
+                bb = work.tile([P, N_TILE], F32)
+                blend(nc, work, f1_raw[:], f2_raw[:], a_rows[:, cols], b_rows[:, cols], v_ps[:], aa[:], bb[:])
+                nc.sync.dma_start(out=out_1[rows, cols], in_=aa[:])
+                nc.sync.dma_start(out=out_2[rows, cols], in_=bb[:])
+
+                num = work.tile([P, N_TILE], F32)
+                den = work.tile([P, N_TILE], F32)
+                blend(nc, work, e1_raw[:], e2_raw[:], a_rows[:, cols], b_rows[:, cols], v_ps[:], num[:], den[:])
+
+                log_den = work.tile([P, N_TILE], F32)
+                nc.scalar.activation(out=log_den[:], in_=den[:], func=FUNC.Ln)
+                inv_den = work.tile([P, N_TILE], F32)
+                nc.scalar.activation(out=inv_den[:], in_=log_den[:], func=FUNC.Exp, scale=-1.0)
+                wkv = work.tile([P, N_TILE], F32)
+                nc.vector.tensor_tensor(out=wkv[:], in0=num[:], in1=inv_den[:], op=ALU.mult)
+                nc.sync.dma_start(out=out_0[rows, cols], in_=wkv[:])

@@ -22,14 +22,20 @@ CHUNKS = DEPTH // P
 ROW_TILES = ROWS // P
 N_TILE = 512
 COL_TILES = WIDTH // N_TILE
+TILES = ROW_TILES * COL_TILES
+HALF = 512
 
 FLOPS = 2 * 2 * ROWS * DEPTH * WIDTH
 
 
-def interleave(copy, grouped, planes):
-    copy(
-        out=grouped.rearrange("p (c i) t -> p c t i", i=4),
-        in_=planes.rearrange("p t (c i) -> p c t i", i=4),
+def interleave(nc, grouped, planes):
+    nc.vector.tensor_copy(
+        out=grouped[:, 0:HALF, :].rearrange("p (c i) t -> p c t i", i=4),
+        in_=planes[:, :, 0:HALF].rearrange("p t (c i) -> p c t i", i=4),
+    )
+    nc.scalar.copy(
+        out=grouped[:, HALF:, :].rearrange("p (c i) t -> p c t i", i=4),
+        in_=planes[:, :, HALF:].rearrange("p t (c i) -> p c t i", i=4),
     )
 
 
@@ -38,23 +44,6 @@ def quantise(nc, grouped, codes, scales):
         out=codes.bitcast(FP8X4),
         scales=scales,
         in_=grouped.rearrange("p c t -> p (c t)"),
-    )
-
-
-def blend(nc, work, old_raw, new_raw, a_cols, b_cols, v_ps, top, bottom):
-    new_v = work.tile([P, N_TILE], F32)
-    nc.vector.scalar_tensor_tensor(
-        out=top, in0=old_raw, scalar=1.0, in1=a_cols, op0=ALU.min, op1=ALU.mult
-    )
-    nc.vector.scalar_tensor_tensor(
-        out=new_v[:], in0=new_raw, scalar=1.0, in1=v_ps, op0=ALU.min, op1=ALU.mult
-    )
-    nc.vector.scalar_tensor_tensor(
-        out=bottom, in0=old_raw, scalar=1.0, in1=b_cols, op0=ALU.min, op1=ALU.mult
-    )
-    nc.vector.tensor_tensor(out=top, in0=top, in1=new_v[:], op=ALU.add)
-    nc.vector.scalar_tensor_tensor(
-        out=bottom, in0=new_raw, scalar=1.0, in1=bottom, op0=ALU.min, op1=ALU.add
     )
 
 
@@ -78,9 +67,9 @@ def tile_rwkv_attention_pa_kernel(
 ):
     nc = tc.nc
     with ExitStack() as pools:
+        pools.enter_context(tc.manual_schedule())
         keep = pools.enter_context(tc.tile_pool(name="keep", bufs=1))
         state = pools.enter_context(tc.tile_pool(name="state", bufs=3))
-        turned = pools.enter_context(tc.psum_pool(name="turned", bufs=2))
         products = pools.enter_context(tc.psum_pool(name="products", bufs=2))
 
         xk_codes = keep.tile([P, PASSES, ROWS], U32, align_bytes=64)
@@ -91,73 +80,84 @@ def tile_rwkv_attention_pa_kernel(
         xv_scales = keep.tile([P, PASSES, ROWS], U8, align_bytes=64)
         wk_scales = keep.tile([P, PASSES, WIDTH], U8, align_bytes=64)
         wv_scales = keep.tile([P, PASSES, WIDTH], U8, align_bytes=64)
-
         decay = keep.tile([P, WIDTH], BF16)
         first = keep.tile([P, WIDTH], BF16)
-
         ident = keep.tile([P, P], BF16)
-        make_identity(nc, ident[:])
-
         mix_rows = keep.tile([P, P], BF16)
-        nc.vector.memset(mix_rows[:], 0.0)
-        nc.sync.dma_start(out=mix_rows[0:CHUNKS, :], in_=k_mixed.rearrange("(c p) -> c p", p=P))
-        nc.sync.dma_start(
-            out=mix_rows[CHUNKS : 2 * CHUNKS, :], in_=v_mixed.rearrange("(c p) -> c p", p=P)
-        )
-        mix_turned = turned.tile([P, P], BF16, tag="x_turned")
-        nc.tensor.transpose(mix_turned[:], mix_rows[:], ident[:])
         mix = keep.tile([P, 2 * CHUNKS], F32)
-        nc.vector.tensor_copy(out=mix[:], in_=mix_turned[:, 0 : 2 * CHUNKS])
         one_minus_mix = keep.tile([P, 2 * CHUNKS], F32)
-        nc.vector.tensor_scalar(
-            out=one_minus_mix[:], in0=mix[:], scalar1=-1.0, scalar2=1.0, op0=ALU.mult, op1=ALU.add
-        )
+
+        def load_state(r):
+            rows = slice(r * P, (r + 1) * P)
+            p_rows = state.tile([P, WIDTH], BF16)
+            a_rows = state.tile([P, WIDTH], BF16)
+            b_rows = state.tile([P, WIDTH], BF16)
+            nc.sync.dma_start(out=p_rows[:], in_=saved_p[rows, :])
+            nc.sync.dma_start(out=a_rows[:], in_=saved_a[rows, :])
+            nc.sync.dma_start(out=b_rows[:], in_=saved_b[rows, :])
+            return p_rows, a_rows, b_rows
 
         with ExitStack() as operand_pools:
             whole = operand_pools.enter_context(tc.tile_pool(name="whole", bufs=1))
-            raw = operand_pools.enter_context(tc.tile_pool(name="raw", bufs=4))
             stage = operand_pools.enter_context(tc.tile_pool(name="stage", bufs=2))
-            group = operand_pools.enter_context(tc.tile_pool(name="group", bufs=3))
+            group = operand_pools.enter_context(tc.tile_pool(name="group", bufs=4))
+            turned = operand_pools.enter_context(tc.psum_pool(name="turned", bufs=2))
 
+            nc.vector.memset(mix_rows[:], 0.0)
+            nc.sync.dma_start(out=mix_rows[0:CHUNKS, :], in_=k_mixed.rearrange("(c p) -> c p", p=P))
+            nc.sync.dma_start(
+                out=mix_rows[CHUNKS : 2 * CHUNKS, :], in_=v_mixed.rearrange("(c p) -> c p", p=P)
+            )
             x_rows = whole.tile([P, ROW_TILES, DEPTH], BF16)
             s_rows = whole.tile([P, ROW_TILES, DEPTH], BF16)
+            wk_planes = whole.tile([P, PASSES, PACK, WIDTH], BF16)
+            wv_planes = whole.tile([P, PASSES, PACK, WIDTH], BF16)
             x_view = x.rearrange("(r p) d -> p r d", p=P)
             s_view = saved_x.rearrange("(r p) d -> p r d", p=P)
             wk_view = key_weight.rearrange("(g t p) a -> g p t a", t=PACK, p=P)
             wv_view = value_weight.rearrange("(g t p) a -> g p t a", t=PACK, p=P)
-
+            nc.sync.dma_start(out=wk_planes[:, 0], in_=wk_view[0])
+            nc.sync.dma_start(out=wv_planes[:, 0], in_=wv_view[0])
             for g in range(PASSES):
                 depth = slice(g * K_PASS, (g + 1) * K_PASS)
-
-                for view, codes, scales in (
-                    (wk_view, wk_codes, wk_scales),
-                    (wv_view, wv_codes, wv_scales),
-                ):
-                    w_planes = raw.tile([P, PACK, WIDTH], BF16)
-                    nc.sync.dma_start(out=w_planes[:], in_=view[g])
-                    w_grouped = group.tile([P, WIDTH, PACK], BF16, tag="grouped", align_bytes=64)
-                    interleave(nc.vector.tensor_copy, w_grouped[:], w_planes[:])
-                    quantise(nc, w_grouped[:], codes[:, g, :], scales[:, g, :])
-
-                nc.sync.dma_start(out=x_rows[:, :, depth], in_=x_view[:, :, depth])
                 nc.sync.dma_start(out=s_rows[:, :, depth], in_=s_view[:, :, depth])
+                nc.sync.dma_start(out=x_rows[:, :, depth], in_=x_view[:, :, depth])
+            nc.sync.dma_start(out=wk_planes[:, 1], in_=wk_view[1])
+            nc.sync.dma_start(out=wv_planes[:, 1], in_=wv_view[1])
+            nc.sync.dma_start(out=decay[:], in_=time_decay.partition_broadcast(P))
+            nc.sync.dma_start(out=first[:], in_=time_first.partition_broadcast(P))
+            loaded = {0: load_state(0), 1: load_state(1)}
+
+            make_identity(nc, ident[:])
+            mix_turned = turned.tile([P, P], BF16, tag="x_turned")
+            nc.tensor.transpose(mix_turned[:], mix_rows[:], ident[:])
+            nc.vector.tensor_copy(out=mix[:], in_=mix_turned[:, 0 : 2 * CHUNKS])
+            nc.vector.tensor_scalar(
+                out=one_minus_mix[:], in0=mix[:], scalar1=-1.0, scalar2=1.0, op0=ALU.mult, op1=ALU.add
+            )
+
+            def quantise_pair(g, k_source, v_source, k_codes, k_scales, v_codes, v_scales):
+                k_grouped = group.tile([P, WIDTH, PACK], BF16, tag="grouped", align_bytes=64)
+                v_grouped = group.tile([P, WIDTH, PACK], BF16, tag="grouped", align_bytes=64)
+                interleave(nc, k_grouped[:], k_source)
+                interleave(nc, v_grouped[:], v_source)
+                quantise(nc, k_grouped[:], k_codes[:, g, :], k_scales[:, g, :])
+                quantise(nc, v_grouped[:], v_codes[:, g, :], v_scales[:, g, :])
+
+            def mix_pass(g):
                 k_planes = stage.tile([P, PACK, ROWS], BF16)
                 v_planes = stage.tile([P, PACK, ROWS], BF16)
                 for t in range(PACK):
                     c = g * PACK + t
-                    x_turned = turned.tile([P, ROWS], BF16)
                     s_turned = turned.tile([P, ROWS], BF16)
+                    x_turned = turned.tile([P, ROWS], BF16)
                     for r in range(ROW_TILES):
                         nc.tensor.transpose(
-                            x_turned[:, r * P : (r + 1) * P],
-                            x_rows[:, r, c * P : (c + 1) * P],
-                            ident[:],
+                            s_turned[:, r * P : (r + 1) * P], s_rows[:, r, c * P : (c + 1) * P], ident[:]
                         )
                     for r in range(ROW_TILES):
                         nc.tensor.transpose(
-                            s_turned[:, r * P : (r + 1) * P],
-                            s_rows[:, r, c * P : (c + 1) * P],
-                            ident[:],
+                            x_turned[:, r * P : (r + 1) * P], x_rows[:, r, c * P : (c + 1) * P], ident[:]
                         )
                     for planes, col in ((k_planes, c), (v_planes, CHUNKS + c)):
                         old_part = stage.tile([P, ROWS], F32)
@@ -175,82 +175,121 @@ def tile_rwkv_attention_pa_kernel(
                             op0=ALU.mult,
                             op1=ALU.add,
                         )
-                for planes, codes, scales in (
-                    (k_planes, xk_codes, xk_scales),
-                    (v_planes, xv_codes, xv_scales),
-                ):
-                    x_grouped = group.tile([P, ROWS, PACK], BF16, tag="grouped", align_bytes=64)
-                    interleave(nc.scalar.copy, x_grouped[:], planes[:])
-                    quantise(nc, x_grouped[:], codes[:, g, :], scales[:, g, :])
+                return k_planes, v_planes
 
-        nc.sync.dma_start(out=decay[:], in_=time_decay.partition_broadcast(P))
-        nc.sync.dma_start(out=first[:], in_=time_first.partition_broadcast(P))
+            for g in range(PASSES):
+                quantise_pair(
+                    g, wk_planes[:, g], wv_planes[:, g], wk_codes, wk_scales, wv_codes, wv_scales
+                )
+                k_planes, v_planes = mix_pass(g)
+                quantise_pair(g, k_planes[:], v_planes[:], xk_codes, xk_scales, xv_codes, xv_scales)
 
         work = pools.enter_context(tc.tile_pool(name="work", bufs=3))
-        for r in range(ROW_TILES):
-            rows = slice(r * P, (r + 1) * P)
-            a_rows = state.tile([P, WIDTH], BF16)
-            b_rows = state.tile([P, WIDTH], BF16)
-            p_rows = state.tile([P, WIDTH], BF16)
-            nc.sync.dma_start(out=p_rows[:], in_=saved_p[rows, :])
-            nc.sync.dma_start(out=a_rows[:], in_=saved_a[rows, :])
-            nc.sync.dma_start(out=b_rows[:], in_=saved_b[rows, :])
-            for h in range(COL_TILES):
-                cols = slice(h * N_TILE, (h + 1) * N_TILE)
 
-                k_ps = products.tile([P, N_TILE], F32)
-                v_ps = products.tile([P, N_TILE], F32)
-                for acc, x_codes, x_scales, w_codes, w_scales in (
-                    (k_ps, xk_codes, xk_scales, wk_codes, wk_scales),
-                    (v_ps, xv_codes, xv_scales, wv_codes, wv_scales),
-                ):
-                    for g in range(PASSES):
-                        nc.tensor.matmul_mx(
-                            out=acc[:],
-                            lhsT=x_codes[:, g, rows].bitcast(FP8X4),
-                            lhsT_scale=x_scales[:, g, rows],
-                            rhs=w_codes[:, g, cols].bitcast(FP8X4),
-                            rhs_scale=w_scales[:, g, cols],
-                            start=(g == 0),
-                            stop=(g == PASSES - 1),
-                        )
+        def feed(i):
+            rows = slice((i // COL_TILES) * P, (i // COL_TILES + 1) * P)
+            cols = slice((i % COL_TILES) * N_TILE, (i % COL_TILES + 1) * N_TILE)
+            k_ps = products.tile([P, N_TILE], F32)
+            v_ps = products.tile([P, N_TILE], F32)
+            for acc, x_codes, x_scales, w_codes, w_scales in (
+                (k_ps, xk_codes, xk_scales, wk_codes, wk_scales),
+                (v_ps, xv_codes, xv_scales, wv_codes, wv_scales),
+            ):
+                for g in range(PASSES):
+                    nc.tensor.matmul_mx(
+                        out=acc[:],
+                        lhsT=x_codes[:, g, rows].bitcast(FP8X4),
+                        lhsT_scale=x_scales[:, g, rows],
+                        rhs=w_codes[:, g, cols].bitcast(FP8X4),
+                        rhs_scale=w_scales[:, g, cols],
+                        start=(g == 0),
+                        stop=(g == PASSES - 1),
+                    )
+            return k_ps, v_ps
 
-                lead = work.tile([P, N_TILE], F32)
-                nc.vector.tensor_tensor(out=lead[:], in0=k_ps[:], in1=p_rows[:, cols], op=ALU.subtract)
-                behind = work.tile([P, N_TILE], F32)
-                nc.vector.tensor_tensor(out=behind[:], in0=decay[:, cols], in1=lead[:], op=ALU.subtract)
-                ahead = work.tile([P, N_TILE], F32)
-                nc.vector.tensor_tensor(out=ahead[:], in0=lead[:], in1=first[:, cols], op=ALU.add)
+        def gap(i, k_ps, p_rows):
+            rows = slice((i // COL_TILES) * P, (i // COL_TILES + 1) * P)
+            cols = slice((i % COL_TILES) * N_TILE, (i % COL_TILES + 1) * N_TILE)
+            lead = work.tile([P, N_TILE], F32)
+            behind = work.tile([P, N_TILE], F32)
+            ahead = work.tile([P, N_TILE], F32)
+            p2 = work.tile([P, N_TILE], F32)
+            nc.vector.tensor_tensor(out=lead[:], in0=k_ps[:], in1=p_rows[:, cols], op=ALU.subtract)
+            nc.vector.tensor_tensor(out=behind[:], in0=decay[:, cols], in1=lead[:], op=ALU.subtract)
+            nc.vector.tensor_tensor(out=ahead[:], in0=lead[:], in1=first[:, cols], op=ALU.add)
+            nc.vector.scalar_tensor_tensor(
+                out=p2[:], in0=behind[:], scalar=0.0, in1=k_ps[:], op0=ALU.max, op1=ALU.add
+            )
+            nc.sync.dma_start(out=out_3[rows, cols], in_=p2[:])
+            f1_raw = work.tile([P, N_TILE], F32)
+            f2_raw = work.tile([P, N_TILE], F32)
+            e1_raw = work.tile([P, N_TILE], F32)
+            e2_raw = work.tile([P, N_TILE], F32)
+            nc.scalar.activation(out=f1_raw[:], in_=behind[:], func=FUNC.Exp)
+            nc.scalar.activation(out=f2_raw[:], in_=behind[:], func=FUNC.Exp, scale=-1.0)
+            nc.scalar.activation(out=e1_raw[:], in_=ahead[:], func=FUNC.Exp, scale=-1.0)
+            nc.scalar.activation(out=e2_raw[:], in_=ahead[:], func=FUNC.Exp)
+            return f1_raw, f2_raw, e1_raw, e2_raw
 
-                p2 = work.tile([P, N_TILE], F32)
-                nc.vector.scalar_tensor_tensor(
-                    out=p2[:], in0=behind[:], scalar=0.0, in1=k_ps[:], op0=ALU.max, op1=ALU.add
+        def clamped(out, raw, other, op):
+            nc.vector.scalar_tensor_tensor(
+                out=out[:], in0=raw[:], scalar=1.0, in1=other, op0=ALU.min, op1=op
+            )
+
+        def blend(i, factors, v_ps, a_rows, b_rows):
+            rows = slice((i // COL_TILES) * P, (i // COL_TILES + 1) * P)
+            cols = slice((i % COL_TILES) * N_TILE, (i % COL_TILES + 1) * N_TILE)
+            f1_raw, f2_raw, e1_raw, e2_raw = factors
+            aa = work.tile([P, N_TILE], F32)
+            bb = work.tile([P, N_TILE], F32)
+            num = work.tile([P, N_TILE], F32)
+            den = work.tile([P, N_TILE], F32)
+            f2_v = work.tile([P, N_TILE], F32)
+            e2_v = work.tile([P, N_TILE], F32)
+            clamped(aa, f1_raw, a_rows[:, cols], ALU.mult)
+            clamped(f2_v, f2_raw, v_ps[:], ALU.mult)
+            nc.gpsimd.tensor_tensor(out=aa[:], in0=aa[:], in1=f2_v[:], op=ALU.add)
+            clamped(bb, f1_raw, b_rows[:, cols], ALU.mult)
+            clamped(den, e1_raw, b_rows[:, cols], ALU.mult)
+            clamped(bb, f2_raw, bb[:], ALU.add)
+            clamped(num, e1_raw, a_rows[:, cols], ALU.mult)
+            clamped(e2_v, e2_raw, v_ps[:], ALU.mult)
+            nc.gpsimd.tensor_tensor(out=num[:], in0=num[:], in1=e2_v[:], op=ALU.add)
+            clamped(den, e2_raw, den[:], ALU.add)
+            nc.sync.dma_start(out=out_1[rows, cols], in_=aa[:])
+            nc.sync.dma_start(out=out_2[rows, cols], in_=bb[:])
+            return num, den
+
+        def invert(den):
+            log_den = work.tile([P, N_TILE], F32)
+            inv_den = work.tile([P, N_TILE], F32)
+            nc.scalar.activation(out=log_den[:], in_=den[:], func=FUNC.Ln)
+            nc.scalar.activation(out=inv_den[:], in_=log_den[:], func=FUNC.Exp, scale=-1.0)
+            return inv_den
+
+        def finish(i, num, inv_den):
+            rows = slice((i // COL_TILES) * P, (i // COL_TILES + 1) * P)
+            cols = slice((i % COL_TILES) * N_TILE, (i % COL_TILES + 1) * N_TILE)
+            wkv = work.tile([P, N_TILE], F32)
+            nc.vector.tensor_tensor(out=wkv[:], in0=num[:], in1=inv_den[:], op=ALU.mult)
+            nc.sync.dma_start(out=out_0[rows, cols], in_=wkv[:])
+
+        fed = {0: feed(0), 1: feed(1)}
+        factors = {}
+        fractions = {}
+        for s in range(-1, TILES + 1):
+            if s - 1 >= 0:
+                inv_den = invert(fractions[s - 1][1])
+            if s + 2 < TILES and s + 2 >= 2:
+                fed[s + 2] = feed(s + 2)
+            if s + 1 < TILES:
+                factors[s + 1] = gap(s + 1, fed[s + 1][0], loaded[(s + 1) // COL_TILES][0])
+            if 0 <= s < TILES:
+                fractions[s] = blend(
+                    s, factors[s], fed[s][1], loaded[s // COL_TILES][1], loaded[s // COL_TILES][2]
                 )
-                nc.sync.dma_start(out=out_3[rows, cols], in_=p2[:])
-
-                f1_raw = work.tile([P, N_TILE], F32)
-                f2_raw = work.tile([P, N_TILE], F32)
-                e1_raw = work.tile([P, N_TILE], F32)
-                e2_raw = work.tile([P, N_TILE], F32)
-                nc.scalar.activation(out=f1_raw[:], in_=behind[:], func=FUNC.Exp)
-                nc.scalar.activation(out=f2_raw[:], in_=behind[:], func=FUNC.Exp, scale=-1.0)
-                nc.scalar.activation(out=e1_raw[:], in_=ahead[:], func=FUNC.Exp, scale=-1.0)
-                nc.scalar.activation(out=e2_raw[:], in_=ahead[:], func=FUNC.Exp)
-
-                aa = work.tile([P, N_TILE], F32)
-                bb = work.tile([P, N_TILE], F32)
-                blend(nc, work, f1_raw[:], f2_raw[:], a_rows[:, cols], b_rows[:, cols], v_ps[:], aa[:], bb[:])
-                nc.sync.dma_start(out=out_1[rows, cols], in_=aa[:])
-                nc.sync.dma_start(out=out_2[rows, cols], in_=bb[:])
-
-                num = work.tile([P, N_TILE], F32)
-                den = work.tile([P, N_TILE], F32)
-                blend(nc, work, e1_raw[:], e2_raw[:], a_rows[:, cols], b_rows[:, cols], v_ps[:], num[:], den[:])
-
-                log_den = work.tile([P, N_TILE], F32)
-                nc.scalar.activation(out=log_den[:], in_=den[:], func=FUNC.Ln)
-                inv_den = work.tile([P, N_TILE], F32)
-                nc.scalar.activation(out=inv_den[:], in_=log_den[:], func=FUNC.Exp, scale=-1.0)
-                wkv = work.tile([P, N_TILE], F32)
-                nc.vector.tensor_tensor(out=wkv[:], in0=num[:], in1=inv_den[:], op=ALU.mult)
-                nc.sync.dma_start(out=out_0[rows, cols], in_=wkv[:])
+            if s - 1 >= 0:
+                finish(s - 1, fractions[s - 1][0], inv_den)
+            ahead_rows = (s + 1) // COL_TILES + 2
+            if (s + 1) % COL_TILES == 0 and ahead_rows < ROW_TILES:
+                loaded[ahead_rows] = load_state(ahead_rows)

@@ -248,13 +248,13 @@ def tile_rwkv_attention_pa_kernel(
             e2_v = work.tile([P, N_TILE], F32)
             clamped(aa, f1_raw, a_rows[:, cols], ALU.mult)
             clamped(f2_v, f2_raw, v_ps[:], ALU.mult)
-            nc.gpsimd.tensor_tensor(out=aa[:], in0=aa[:], in1=f2_v[:], op=ALU.add)
             clamped(bb, f1_raw, b_rows[:, cols], ALU.mult)
-            clamped(den, e1_raw, b_rows[:, cols], ALU.mult)
-            clamped(bb, f2_raw, bb[:], ALU.add)
+            nc.vector.tensor_tensor(out=aa[:], in0=aa[:], in1=f2_v[:], op=ALU.add)
             clamped(num, e1_raw, a_rows[:, cols], ALU.mult)
+            clamped(bb, f2_raw, bb[:], ALU.add)
             clamped(e2_v, e2_raw, v_ps[:], ALU.mult)
-            nc.gpsimd.tensor_tensor(out=num[:], in0=num[:], in1=e2_v[:], op=ALU.add)
+            clamped(den, e1_raw, b_rows[:, cols], ALU.mult)
+            nc.vector.tensor_tensor(out=num[:], in0=num[:], in1=e2_v[:], op=ALU.add)
             clamped(den, e2_raw, den[:], ALU.add)
             nc.sync.dma_start(out=out_1[rows, cols], in_=aa[:])
             nc.sync.dma_start(out=out_2[rows, cols], in_=bb[:])

@@ -21,8 +21,12 @@ PASSES = DEPTH // K_PASS
 CHUNKS = DEPTH // P
 ROW_TILES = ROWS // P
 N_TILE = 512
-COL_TILES = WIDTH // N_TILE
-TILES = ROW_TILES * COL_TILES
+ROW_HALVES = ROWS // N_TILE
+BLOCKS = N_TILE // P
+COL_BLOCKS = WIDTH // P
+TILES = ROW_HALVES * COL_BLOCKS
+FACTOR_BANKS = ("f1_ps", "f2_ps", "e1_ps", "e2_ps")
+GROUP = 4
 HALF = 512
 
 FLOPS = 2 * 2 * ROWS * DEPTH * WIDTH
@@ -69,8 +73,6 @@ def tile_rwkv_attention_pa_kernel(
     with ExitStack() as pools:
         pools.enter_context(tc.manual_schedule())
         keep = pools.enter_context(tc.tile_pool(name="keep", bufs=1))
-        state = pools.enter_context(tc.tile_pool(name="state", bufs=3))
-        products = pools.enter_context(tc.psum_pool(name="products", bufs=2))
 
         xk_codes = keep.tile([P, PASSES, ROWS], U32, align_bytes=64)
         xv_codes = keep.tile([P, PASSES, ROWS], U32, align_bytes=64)
@@ -80,22 +82,19 @@ def tile_rwkv_attention_pa_kernel(
         xv_scales = keep.tile([P, PASSES, ROWS], U8, align_bytes=64)
         wk_scales = keep.tile([P, PASSES, WIDTH], U8, align_bytes=64)
         wv_scales = keep.tile([P, PASSES, WIDTH], U8, align_bytes=64)
-        decay = keep.tile([P, WIDTH], BF16)
-        first = keep.tile([P, WIDTH], BF16)
+        p_rows = keep.tile([P, ROW_TILES, WIDTH], BF16)
+        a_rows = keep.tile([P, ROW_TILES, WIDTH], BF16)
+        b_rows = keep.tile([P, ROW_TILES, WIDTH], BF16)
         ident = keep.tile([P, P], BF16)
-        mix_rows = keep.tile([P, P], BF16)
-        mix = keep.tile([P, 2 * CHUNKS], F32)
+        ident_f32 = keep.tile([P, P], F32)
+        vector_rows = keep.tile([P, P], BF16)
+        columns = keep.tile([P, 4 * CHUNKS], F32)
         one_minus_mix = keep.tile([P, 2 * CHUNKS], F32)
-
-        def load_state(r):
-            rows = slice(r * P, (r + 1) * P)
-            p_rows = state.tile([P, WIDTH], BF16)
-            a_rows = state.tile([P, WIDTH], BF16)
-            b_rows = state.tile([P, WIDTH], BF16)
-            nc.sync.dma_start(out=p_rows[:], in_=saved_p[rows, :])
-            nc.sync.dma_start(out=a_rows[:], in_=saved_a[rows, :])
-            nc.sync.dma_start(out=b_rows[:], in_=saved_b[rows, :])
-            return p_rows, a_rows, b_rows
+        shift = keep.tile([P, CHUNKS], F32)
+        minus_shift = keep.tile([P, CHUNKS], F32)
+        mix = columns[:, 0 : 2 * CHUNKS]
+        decay = columns[:, 2 * CHUNKS : 3 * CHUNKS]
+        first = columns[:, 3 * CHUNKS : 4 * CHUNKS]
 
         with ExitStack() as operand_pools:
             whole = operand_pools.enter_context(tc.tile_pool(name="whole", bufs=1))
@@ -103,11 +102,12 @@ def tile_rwkv_attention_pa_kernel(
             group = operand_pools.enter_context(tc.tile_pool(name="group", bufs=4))
             turned = operand_pools.enter_context(tc.psum_pool(name="turned", bufs=2))
 
-            nc.vector.memset(mix_rows[:], 0.0)
-            nc.sync.dma_start(out=mix_rows[0:CHUNKS, :], in_=k_mixed.rearrange("(c p) -> c p", p=P))
-            nc.sync.dma_start(
-                out=mix_rows[CHUNKS : 2 * CHUNKS, :], in_=v_mixed.rearrange("(c p) -> c p", p=P)
-            )
+            nc.vector.memset(vector_rows[:], 0.0)
+            for n, vector in enumerate((k_mixed, v_mixed, time_decay, time_first)):
+                nc.sync.dma_start(
+                    out=vector_rows[n * CHUNKS : (n + 1) * CHUNKS, :],
+                    in_=vector.rearrange("(c p) -> c p", p=P),
+                )
             x_rows = whole.tile([P, ROW_TILES, DEPTH], BF16)
             s_rows = whole.tile([P, ROW_TILES, DEPTH], BF16)
             wk_planes = whole.tile([P, PASSES, PACK, WIDTH], BF16)
@@ -124,17 +124,24 @@ def tile_rwkv_attention_pa_kernel(
                 nc.sync.dma_start(out=x_rows[:, :, depth], in_=x_view[:, :, depth])
             nc.sync.dma_start(out=wk_planes[:, 1], in_=wk_view[1])
             nc.sync.dma_start(out=wv_planes[:, 1], in_=wv_view[1])
-            nc.sync.dma_start(out=decay[:], in_=time_decay.partition_broadcast(P))
-            nc.sync.dma_start(out=first[:], in_=time_first.partition_broadcast(P))
-            loaded = {0: load_state(0), 1: load_state(1)}
+            for h in range(ROW_HALVES):
+                blocks = slice(h * BLOCKS, (h + 1) * BLOCKS)
+                for rows_tile, source in ((p_rows, saved_p), (a_rows, saved_a), (b_rows, saved_b)):
+                    nc.sync.dma_start(
+                        out=rows_tile[:, blocks, :],
+                        in_=source.rearrange("(r p) a -> p r a", p=P)[:, blocks, :],
+                    )
 
             make_identity(nc, ident[:])
-            mix_turned = turned.tile([P, P], BF16, tag="x_turned")
-            nc.tensor.transpose(mix_turned[:], mix_rows[:], ident[:])
-            nc.vector.tensor_copy(out=mix[:], in_=mix_turned[:, 0 : 2 * CHUNKS])
+            make_identity(nc, ident_f32[:])
+            vectors_turned = turned.tile([P, P], BF16, tag="x_turned")
+            nc.tensor.transpose(vectors_turned[:], vector_rows[:], ident[:])
+            nc.vector.tensor_copy(out=columns[:], in_=vectors_turned[:, 0 : 4 * CHUNKS])
             nc.vector.tensor_scalar(
-                out=one_minus_mix[:], in0=mix[:], scalar1=-1.0, scalar2=1.0, op0=ALU.mult, op1=ALU.add
+                out=one_minus_mix[:], in0=mix, scalar1=-1.0, scalar2=1.0, op0=ALU.mult, op1=ALU.add
             )
+            nc.vector.tensor_tensor(out=shift[:], in0=decay, in1=first, op=ALU.add)
+            nc.vector.tensor_scalar_mul(out=minus_shift[:], in0=shift[:], scalar1=-1.0)
 
             def quantise_pair(g, k_source, v_source, k_codes, k_scales, v_codes, v_scales):
                 k_grouped = group.tile([P, WIDTH, PACK], BF16, tag="grouped", align_bytes=64)
@@ -184,112 +191,172 @@ def tile_rwkv_attention_pa_kernel(
                 k_planes, v_planes = mix_pass(g)
                 quantise_pair(g, k_planes[:], v_planes[:], xk_codes, xk_scales, xv_codes, xv_scales)
 
-        work = pools.enter_context(tc.tile_pool(name="work", bufs=3))
+        work = pools.enter_context(tc.tile_pool(name="work", bufs=2))
+        banks = pools.enter_context(tc.psum_pool(name="banks", bufs=1))
 
-        def feed(i):
-            rows = slice((i // COL_TILES) * P, (i // COL_TILES + 1) * P)
-            cols = slice((i % COL_TILES) * N_TILE, (i % COL_TILES + 1) * N_TILE)
-            k_ps = products.tile([P, N_TILE], F32)
-            v_ps = products.tile([P, N_TILE], F32)
-            for acc, x_codes, x_scales, w_codes, w_scales in (
-                (k_ps, xk_codes, xk_scales, wk_codes, wk_scales),
-                (v_ps, xv_codes, xv_scales, wv_codes, wv_scales),
-            ):
+        def rows_of(i, b=0, count=BLOCKS):
+            first_row = (i // COL_BLOCKS) * N_TILE + b * P
+            return slice(first_row, first_row + count * P)
+
+        def blocks_of(i):
+            return slice((i // COL_BLOCKS) * BLOCKS, (i // COL_BLOCKS + 1) * BLOCKS)
+
+        def cols_of(i, count=1):
+            return slice((i % COL_BLOCKS) * P, (i % COL_BLOCKS + count) * P)
+
+        def turn(i):
+            p_turned = banks.tile([P, N_TILE], BF16)
+            for b in range(BLOCKS):
+                nc.tensor.transpose(
+                    p_turned[:, b * P : (b + 1) * P],
+                    p_rows[:, (i // COL_BLOCKS) * BLOCKS + b, cols_of(i)],
+                    ident[:],
+                )
+            k_turned = banks.tile([P, N_TILE], F32)
+            for g in range(PASSES):
+                nc.tensor.matmul_mx(
+                    out=k_turned[:],
+                    lhsT=wk_codes[:, g, cols_of(i)].bitcast(FP8X4),
+                    lhsT_scale=wk_scales[:, g, cols_of(i)],
+                    rhs=xk_codes[:, g, rows_of(i)].bitcast(FP8X4),
+                    rhs_scale=xk_scales[:, g, rows_of(i)],
+                    start=(g == 0),
+                    stop=(g == PASSES - 1),
+                )
+            p_cols = work.tile([P, N_TILE], BF16)
+            nc.scalar.copy(out=p_cols[:], in_=p_turned[:])
+            return p_cols, k_turned
+
+        def gap(i, p_cols, k_turned):
+            j = i % COL_BLOCKS
+            behind = work.tile([P, N_TILE], F32)
+            p2_turned = work.tile([P, N_TILE], F32)
+            for out, op in ((behind, ALU.subtract), (p2_turned, ALU.max)):
+                nc.vector.scalar_tensor_tensor(
+                    out=out[:],
+                    in0=p_cols[:],
+                    scalar=decay[:, j : j + 1],
+                    in1=k_turned[:],
+                    op0=ALU.add,
+                    op1=op,
+                )
+            f1_raw = work.tile([P, N_TILE], F32, bufs=3)
+            f2_raw = work.tile([P, N_TILE], F32, bufs=3)
+            e1_raw = work.tile([P, N_TILE], F32, bufs=3)
+            e2_raw = work.tile([P, N_TILE], F32, bufs=3)
+            nc.scalar.activation(out=f1_raw[:], in_=behind[:], func=FUNC.Exp)
+            nc.scalar.activation(out=f2_raw[:], in_=behind[:], func=FUNC.Exp, scale=-1.0)
+            nc.scalar.activation(
+                out=e1_raw[:], in_=behind[:], func=FUNC.Exp, bias=minus_shift[:, j : j + 1]
+            )
+            nc.scalar.activation(
+                out=e2_raw[:], in_=behind[:], func=FUNC.Exp, scale=-1.0, bias=shift[:, j : j + 1]
+            )
+            return p2_turned, (f1_raw, f2_raw, e1_raw, e2_raw)
+
+        def upright(turned_tile, name):
+            bank = banks.tile([P, BLOCKS, P], F32, name=name)
+            for b in range(BLOCKS):
+                nc.tensor.transpose(bank[:, b, :], turned_tile[:, b * P : (b + 1) * P], ident_f32[:])
+            return bank
+
+        def project_v(i):
+            v_ps = banks.tile([P, BLOCKS, P], F32)
+            for b in range(BLOCKS):
+                rows = rows_of(i, b, 1)
                 for g in range(PASSES):
                     nc.tensor.matmul_mx(
-                        out=acc[:],
-                        lhsT=x_codes[:, g, rows].bitcast(FP8X4),
-                        lhsT_scale=x_scales[:, g, rows],
-                        rhs=w_codes[:, g, cols].bitcast(FP8X4),
-                        rhs_scale=w_scales[:, g, cols],
+                        out=v_ps[:, b, :],
+                        lhsT=xv_codes[:, g, rows].bitcast(FP8X4),
+                        lhsT_scale=xv_scales[:, g, rows],
+                        rhs=wv_codes[:, g, cols_of(i)].bitcast(FP8X4),
+                        rhs_scale=wv_scales[:, g, cols_of(i)],
                         start=(g == 0),
                         stop=(g == PASSES - 1),
                     )
-            return k_ps, v_ps
-
-        def gap(i, k_ps, p_rows):
-            rows = slice((i // COL_TILES) * P, (i // COL_TILES + 1) * P)
-            cols = slice((i % COL_TILES) * N_TILE, (i % COL_TILES + 1) * N_TILE)
-            lead = work.tile([P, N_TILE], F32)
-            behind = work.tile([P, N_TILE], F32)
-            ahead = work.tile([P, N_TILE], F32)
-            p2 = work.tile([P, N_TILE], F32)
-            nc.vector.tensor_tensor(out=lead[:], in0=k_ps[:], in1=p_rows[:, cols], op=ALU.subtract)
-            nc.vector.tensor_tensor(out=behind[:], in0=decay[:, cols], in1=lead[:], op=ALU.subtract)
-            nc.vector.tensor_tensor(out=ahead[:], in0=lead[:], in1=first[:, cols], op=ALU.add)
-            nc.vector.scalar_tensor_tensor(
-                out=p2[:], in0=behind[:], scalar=0.0, in1=k_ps[:], op0=ALU.max, op1=ALU.add
-            )
-            nc.sync.dma_start(out=out_3[rows, cols], in_=p2[:])
-            f1_raw = work.tile([P, N_TILE], F32)
-            f2_raw = work.tile([P, N_TILE], F32)
-            e1_raw = work.tile([P, N_TILE], F32)
-            e2_raw = work.tile([P, N_TILE], F32)
-            nc.scalar.activation(out=f1_raw[:], in_=behind[:], func=FUNC.Exp)
-            nc.scalar.activation(out=f2_raw[:], in_=behind[:], func=FUNC.Exp, scale=-1.0)
-            nc.scalar.activation(out=e1_raw[:], in_=ahead[:], func=FUNC.Exp, scale=-1.0)
-            nc.scalar.activation(out=e2_raw[:], in_=ahead[:], func=FUNC.Exp)
-            return f1_raw, f2_raw, e1_raw, e2_raw
+            v_rows = work.tile([P, BLOCKS, P], F32)
+            nc.scalar.copy(out=v_rows[:], in_=v_ps[:])
+            return v_rows
 
         def clamped(out, raw, other, op):
             nc.vector.scalar_tensor_tensor(
-                out=out[:], in0=raw[:], scalar=1.0, in1=other, op0=ALU.min, op1=op
+                out=out, in0=raw[:], scalar=1.0, in1=other, op0=ALU.min, op1=op
             )
 
-        def blend(i, factors, v_ps, a_rows, b_rows):
-            rows = slice((i // COL_TILES) * P, (i // COL_TILES + 1) * P)
-            cols = slice((i % COL_TILES) * N_TILE, (i % COL_TILES + 1) * N_TILE)
-            f1_raw, f2_raw, e1_raw, e2_raw = factors
-            aa = work.tile([P, N_TILE], F32)
-            bb = work.tile([P, N_TILE], F32)
-            num = work.tile([P, N_TILE], F32)
-            den = work.tile([P, N_TILE], F32)
-            f2_v = work.tile([P, N_TILE], F32)
-            e2_v = work.tile([P, N_TILE], F32)
-            clamped(aa, f1_raw, a_rows[:, cols], ALU.mult)
-            clamped(f2_v, f2_raw, v_ps[:], ALU.mult)
-            clamped(bb, f1_raw, b_rows[:, cols], ALU.mult)
-            nc.vector.tensor_tensor(out=aa[:], in0=aa[:], in1=f2_v[:], op=ALU.add)
-            clamped(num, e1_raw, a_rows[:, cols], ALU.mult)
-            clamped(bb, f2_raw, bb[:], ALU.add)
-            clamped(e2_v, e2_raw, v_ps[:], ALU.mult)
-            clamped(den, e1_raw, b_rows[:, cols], ALU.mult)
-            nc.vector.tensor_tensor(out=num[:], in0=num[:], in1=e2_v[:], op=ALU.add)
-            clamped(den, e2_raw, den[:], ALU.add)
-            nc.sync.dma_start(out=out_1[rows, cols], in_=aa[:])
-            nc.sync.dma_start(out=out_2[rows, cols], in_=bb[:])
-            return num, den
+        def blend(i, factor_banks, v_rows, aa, bb, num, den):
+            f1_ps, f2_ps, e1_ps, e2_ps = factor_banks
+            a_part = a_rows[:, blocks_of(i), cols_of(i)]
+            b_part = b_rows[:, blocks_of(i), cols_of(i)]
+            f2_v = work.tile([P, BLOCKS, P], F32)
+            e2_v = work.tile([P, BLOCKS, P], F32)
+            clamped(aa, f1_ps, a_part, ALU.mult)
+            clamped(bb, f1_ps, b_part, ALU.mult)
+            clamped(f2_v[:], f2_ps, v_rows[:], ALU.mult)
+            clamped(bb, f2_ps, bb, ALU.add)
+            nc.gpsimd.tensor_tensor(out=aa, in0=aa, in1=f2_v[:], op=ALU.add)
+            clamped(num, e1_ps, a_part, ALU.mult)
+            clamped(den, e1_ps, b_part, ALU.mult)
+            clamped(e2_v[:], e2_ps, v_rows[:], ALU.mult)
+            clamped(den, e2_ps, den, ALU.add)
+            nc.gpsimd.tensor_tensor(out=num, in0=num, in1=e2_v[:], op=ALU.add)
 
-        def invert(den):
-            log_den = work.tile([P, N_TILE], F32)
-            inv_den = work.tile([P, N_TILE], F32)
-            nc.scalar.activation(out=log_den[:], in_=den[:], func=FUNC.Ln)
-            nc.scalar.activation(out=inv_den[:], in_=log_den[:], func=FUNC.Exp, scale=-1.0)
-            return inv_den
+        def store(out, group_tile, q):
+            first_tile = q * GROUP
+            nc.sync.dma_start(
+                out=out.rearrange("(r p) a -> p r a", p=P)[
+                    :, blocks_of(first_tile), cols_of(first_tile, GROUP)
+                ],
+                in_=group_tile[:].rearrange("p b n c -> p b (n c)"),
+            )
 
-        def finish(i, num, inv_den):
-            rows = slice((i // COL_TILES) * P, (i // COL_TILES + 1) * P)
-            cols = slice((i % COL_TILES) * N_TILE, (i % COL_TILES + 1) * N_TILE)
-            wkv = work.tile([P, N_TILE], F32)
-            nc.vector.tensor_tensor(out=wkv[:], in0=num[:], in1=inv_den[:], op=ALU.mult)
-            nc.sync.dma_start(out=out_0[rows, cols], in_=wkv[:])
-
-        fed = {0: feed(0), 1: feed(1)}
-        factors = {}
-        fractions = {}
-        for s in range(-1, TILES + 1):
-            if s - 1 >= 0:
-                inv_den = invert(fractions[s - 1][1])
-            if s + 2 < TILES and s + 2 >= 2:
-                fed[s + 2] = feed(s + 2)
-            if s + 1 < TILES:
-                factors[s + 1] = gap(s + 1, fed[s + 1][0], loaded[(s + 1) // COL_TILES][0])
+        turned_in = {0: turn(0)}
+        raw = {}
+        v_in = {}
+        factor_in = {}
+        grouped_out = {}
+        for s in range(-2, TILES + 1):
+            if s + 2 < TILES:
+                i = s + 2
+                if i % GROUP == 0:
+                    p2_group = work.tile([P, BLOCKS, GROUP, P], F32)
+                p2_turned, raw[i] = gap(i, turned_in[i][0], turned_in[i][1])
+            if 0 <= s + 1 < TILES:
+                v_in[s + 1] = project_v(s + 1)
+            if s + 3 < TILES:
+                turned_in[s + 3] = turn(s + 3)
+            if s + 2 < TILES:
+                i = s + 2
+                p2_ps = upright(p2_turned, "p2_ps")
+                nc.scalar.copy(out=p2_group[:, :, i % GROUP, :], in_=p2_ps[:])
+                if i % GROUP == GROUP - 1:
+                    store(out_3, p2_group, i // GROUP)
             if 0 <= s < TILES:
-                fractions[s] = blend(
-                    s, factors[s], fed[s][1], loaded[s // COL_TILES][1], loaded[s // COL_TILES][2]
+                n = s % GROUP
+                if n == 0:
+                    aa_group = work.tile([P, BLOCKS, GROUP, P], F32)
+                    bb_group = work.tile([P, BLOCKS, GROUP, P], F32)
+                    num_group = work.tile([P, BLOCKS, GROUP, P], F32)
+                    den_group = work.tile([P, BLOCKS, GROUP, P], F32)
+                    grouped_out[s // GROUP] = (num_group, den_group)
+                blend(
+                    s,
+                    factor_in[s],
+                    v_in[s],
+                    aa_group[:, :, n, :],
+                    bb_group[:, :, n, :],
+                    num_group[:, :, n, :],
+                    den_group[:, :, n, :],
                 )
-            if s - 1 >= 0:
-                finish(s - 1, fractions[s - 1][0], inv_den)
-            ahead_rows = (s + 1) // COL_TILES + 2
-            if (s + 1) % COL_TILES == 0 and ahead_rows < ROW_TILES:
-                loaded[ahead_rows] = load_state(ahead_rows)
+                if n == GROUP - 1:
+                    store(out_1, aa_group, s // GROUP)
+                    store(out_2, bb_group, s // GROUP)
+            if 0 <= s + 1 < TILES:
+                factor_in[s + 1] = [
+                    upright(raw[s + 1][n], name) for n, name in enumerate(FACTOR_BANKS)
+                ]
+            if s >= GROUP and s % GROUP == 0:
+                num_done, den_done = grouped_out[s // GROUP - 1]
+                nc.scalar.activation(out=den_done[:], in_=den_done[:], func=FUNC.Ln)
+                nc.scalar.activation(out=den_done[:], in_=den_done[:], func=FUNC.Exp, scale=-1.0)
+                nc.gpsimd.tensor_tensor(out=num_done[:], in0=num_done[:], in1=den_done[:], op=ALU.mult)
+                store(out_0, num_done, s // GROUP - 1)

@@ -25,21 +25,22 @@ ROW_HALVES = ROWS // N_TILE
 BLOCKS = N_TILE // P
 COL_BLOCKS = WIDTH // P
 TILES = ROW_HALVES * COL_BLOCKS
-FACTOR_BANKS = ("f1_ps", "f2_ps", "e1_ps", "e2_ps")
+FACTOR_BANKS = ("e1_ps", "e2_ps", "f1_ps", "f2_ps")
 GROUP = 4
-HALF = 512
+VECTOR_SHARE = 640
+assert BLOCKS == GROUP
 
 FLOPS = 2 * 2 * ROWS * DEPTH * WIDTH
 
 
 def interleave(nc, grouped, planes):
     nc.vector.tensor_copy(
-        out=grouped[:, 0:HALF, :].rearrange("p (c i) t -> p c t i", i=4),
-        in_=planes[:, :, 0:HALF].rearrange("p t (c i) -> p c t i", i=4),
+        out=grouped[:, 0:VECTOR_SHARE, :].rearrange("p (c i) t -> p c t i", i=4),
+        in_=planes[:, :, 0:VECTOR_SHARE].rearrange("p t (c i) -> p c t i", i=4),
     )
     nc.scalar.copy(
-        out=grouped[:, HALF:, :].rearrange("p (c i) t -> p c t i", i=4),
-        in_=planes[:, :, HALF:].rearrange("p t (c i) -> p c t i", i=4),
+        out=grouped[:, VECTOR_SHARE:, :].rearrange("p (c i) t -> p c t i", i=4),
+        in_=planes[:, :, VECTOR_SHARE:].rearrange("p t (c i) -> p c t i", i=4),
     )
 
 
@@ -73,6 +74,7 @@ def tile_rwkv_attention_pa_kernel(
     with ExitStack() as pools:
         pools.enter_context(tc.manual_schedule())
         keep = pools.enter_context(tc.tile_pool(name="keep", bufs=1))
+        early = pools.enter_context(tc.psum_pool(name="early", bufs=1))
 
         xk_codes = keep.tile([P, PASSES, ROWS], U32, align_bytes=64)
         xv_codes = keep.tile([P, PASSES, ROWS], U32, align_bytes=64)
@@ -82,9 +84,8 @@ def tile_rwkv_attention_pa_kernel(
         xv_scales = keep.tile([P, PASSES, ROWS], U8, align_bytes=64)
         wk_scales = keep.tile([P, PASSES, WIDTH], U8, align_bytes=64)
         wv_scales = keep.tile([P, PASSES, WIDTH], U8, align_bytes=64)
-        p_rows = keep.tile([P, ROW_TILES, WIDTH], BF16)
-        a_rows = keep.tile([P, ROW_TILES, WIDTH], BF16)
-        b_rows = keep.tile([P, ROW_TILES, WIDTH], BF16)
+        decayed = keep.tile([P, ROW_TILES, WIDTH], F32)
+        decay_rows = keep.tile([P, WIDTH], BF16)
         ident = keep.tile([P, P], BF16)
         ident_f32 = keep.tile([P, P], F32)
         vector_rows = keep.tile([P, P], BF16)
@@ -112,6 +113,7 @@ def tile_rwkv_attention_pa_kernel(
             s_rows = whole.tile([P, ROW_TILES, DEPTH], BF16)
             wk_planes = whole.tile([P, PASSES, PACK, WIDTH], BF16)
             wv_planes = whole.tile([P, PASSES, PACK, WIDTH], BF16)
+            p_rows = whole.tile([P, ROW_TILES, WIDTH], BF16)
             x_view = x.rearrange("(r p) d -> p r d", p=P)
             s_view = saved_x.rearrange("(r p) d -> p r d", p=P)
             wk_view = key_weight.rearrange("(g t p) a -> g p t a", t=PACK, p=P)
@@ -124,16 +126,15 @@ def tile_rwkv_attention_pa_kernel(
                 nc.sync.dma_start(out=x_rows[:, :, depth], in_=x_view[:, :, depth])
             nc.sync.dma_start(out=wk_planes[:, 1], in_=wk_view[1])
             nc.sync.dma_start(out=wv_planes[:, 1], in_=wv_view[1])
-            for h in range(ROW_HALVES):
-                blocks = slice(h * BLOCKS, (h + 1) * BLOCKS)
-                for rows_tile, source in ((p_rows, saved_p), (a_rows, saved_a), (b_rows, saved_b)):
-                    nc.sync.dma_start(
-                        out=rows_tile[:, blocks, :],
-                        in_=source.rearrange("(r p) a -> p r a", p=P)[:, blocks, :],
-                    )
+            nc.sync.dma_start(out=decay_rows[:], in_=time_decay.partition_broadcast(P))
+            nc.sync.dma_start(out=p_rows[:], in_=saved_p.rearrange("(r p) a -> p r a", p=P))
 
             make_identity(nc, ident[:])
             make_identity(nc, ident_f32[:])
+            for r in range(ROW_TILES):
+                nc.gpsimd.tensor_tensor(
+                    out=decayed[:, r, :], in0=p_rows[:, r, :], in1=decay_rows[:], op=ALU.add
+                )
             vectors_turned = turned.tile([P, P], BF16, tag="x_turned")
             nc.tensor.transpose(vectors_turned[:], vector_rows[:], ident[:])
             nc.vector.tensor_copy(out=columns[:], in_=vectors_turned[:, 0 : 4 * CHUNKS])
@@ -191,8 +192,18 @@ def tile_rwkv_attention_pa_kernel(
                 k_planes, v_planes = mix_pass(g)
                 quantise_pair(g, k_planes[:], v_planes[:], xk_codes, xk_scales, xv_codes, xv_scales)
 
-        work = pools.enter_context(tc.tile_pool(name="work", bufs=2))
-        banks = pools.enter_context(tc.psum_pool(name="banks", bufs=1))
+        late = pools.enter_context(tc.tile_pool(name="late", bufs=1, reuse_waits="tile"))
+        work = pools.enter_context(tc.tile_pool(name="work", bufs=2, reuse_waits="tile"))
+        banks = pools.enter_context(tc.psum_pool(name="banks", bufs=1, reuse_waits="tile"))
+        a_rows = late.tile([P, ROW_TILES, WIDTH], BF16)
+        b_rows = late.tile([P, ROW_TILES, WIDTH], BF16)
+        for h in range(ROW_HALVES):
+            blocks = slice(h * BLOCKS, (h + 1) * BLOCKS)
+            for rows_tile, source in ((a_rows, saved_a), (b_rows, saved_b)):
+                nc.sync.dma_start(
+                    out=rows_tile[:, blocks, :],
+                    in_=source.rearrange("(r p) a -> p r a", p=P)[:, blocks, :],
+                )
 
         def rows_of(i, b=0, count=BLOCKS):
             first_row = (i // COL_BLOCKS) * N_TILE + b * P
@@ -204,55 +215,50 @@ def tile_rwkv_attention_pa_kernel(
         def cols_of(i, count=1):
             return slice((i % COL_BLOCKS) * P, (i % COL_BLOCKS + count) * P)
 
-        def turn(i):
-            p_turned = banks.tile([P, N_TILE], BF16)
-            for b in range(BLOCKS):
-                nc.tensor.transpose(
-                    p_turned[:, b * P : (b + 1) * P],
-                    p_rows[:, (i // COL_BLOCKS) * BLOCKS + b, cols_of(i)],
-                    ident[:],
-                )
-            k_turned = banks.tile([P, N_TILE], F32)
-            for g in range(PASSES):
-                nc.tensor.matmul_mx(
-                    out=k_turned[:],
-                    lhsT=wk_codes[:, g, cols_of(i)].bitcast(FP8X4),
-                    lhsT_scale=wk_scales[:, g, cols_of(i)],
-                    rhs=xk_codes[:, g, rows_of(i)].bitcast(FP8X4),
-                    rhs_scale=xk_scales[:, g, rows_of(i)],
-                    start=(g == 0),
-                    stop=(g == PASSES - 1),
-                )
-            p_cols = work.tile([P, N_TILE], BF16)
-            nc.scalar.copy(out=p_cols[:], in_=p_turned[:])
-            return p_cols, k_turned
+        def project(i):
+            k_ps = early.tile([P, BLOCKS, P], F32)
+            v_ps = early.tile([P, BLOCKS, P], F32)
+            for acc, x_codes, x_scales, w_codes, w_scales in (
+                (k_ps, xk_codes, xk_scales, wk_codes, wk_scales),
+                (v_ps, xv_codes, xv_scales, wv_codes, wv_scales),
+            ):
+                for b in range(BLOCKS):
+                    for g in range(PASSES):
+                        nc.tensor.matmul_mx(
+                            out=acc[:, b, :],
+                            lhsT=x_codes[:, g, rows_of(i, b, 1)].bitcast(FP8X4),
+                            lhsT_scale=x_scales[:, g, rows_of(i, b, 1)],
+                            rhs=w_codes[:, g, cols_of(i)].bitcast(FP8X4),
+                            rhs_scale=w_scales[:, g, cols_of(i)],
+                            start=(g == 0),
+                            stop=(g == PASSES - 1),
+                        )
+            v_rows = work.tile([P, BLOCKS, P], F32, bufs=4)
+            nc.scalar.copy(out=v_rows[:], in_=v_ps[:])
+            return k_ps, v_rows
 
-        def gap(i, p_cols, k_turned):
+        def compare(i, k_ps, p2):
             j = i % COL_BLOCKS
-            behind = work.tile([P, N_TILE], F32)
-            p2_turned = work.tile([P, N_TILE], F32)
-            for out, op in ((behind, ALU.subtract), (p2_turned, ALU.max)):
-                nc.vector.scalar_tensor_tensor(
-                    out=out[:],
-                    in0=p_cols[:],
-                    scalar=decay[:, j : j + 1],
-                    in1=k_turned[:],
-                    op0=ALU.add,
-                    op1=op,
-                )
-            f1_raw = work.tile([P, N_TILE], F32, bufs=3)
-            f2_raw = work.tile([P, N_TILE], F32, bufs=3)
-            e1_raw = work.tile([P, N_TILE], F32, bufs=3)
-            e2_raw = work.tile([P, N_TILE], F32, bufs=3)
-            nc.scalar.activation(out=f1_raw[:], in_=behind[:], func=FUNC.Exp)
-            nc.scalar.activation(out=f2_raw[:], in_=behind[:], func=FUNC.Exp, scale=-1.0)
+            decayed_part = decayed[:, blocks_of(i), cols_of(i)]
+            lead = work.tile([P, BLOCKS, P], F32)
+            nc.vector.tensor_tensor(out=lead[:], in0=k_ps[:], in1=decayed_part, op=ALU.subtract)
+            nc.vector.tensor_tensor(out=p2, in0=k_ps[:], in1=decayed_part, op=ALU.max)
+            lead_turned = early.tile([P, N_TILE], F32)
+            for b in range(BLOCKS):
+                nc.tensor.transpose(lead_turned[:, b * P : (b + 1) * P], lead[:, b, :], ident_f32[:])
+            e1_raw = work.tile([P, N_TILE], F32)
+            e2_raw = work.tile([P, N_TILE], F32)
+            f1_raw = work.tile([P, N_TILE], F32)
+            f2_raw = work.tile([P, N_TILE], F32)
             nc.scalar.activation(
-                out=e1_raw[:], in_=behind[:], func=FUNC.Exp, bias=minus_shift[:, j : j + 1]
+                out=e1_raw[:], in_=lead_turned[:], func=FUNC.Exp, scale=-1.0, bias=minus_shift[:, j : j + 1]
             )
             nc.scalar.activation(
-                out=e2_raw[:], in_=behind[:], func=FUNC.Exp, scale=-1.0, bias=shift[:, j : j + 1]
+                out=e2_raw[:], in_=lead_turned[:], func=FUNC.Exp, bias=shift[:, j : j + 1]
             )
-            return p2_turned, (f1_raw, f2_raw, e1_raw, e2_raw)
+            nc.scalar.activation(out=f1_raw[:], in_=lead_turned[:], func=FUNC.Exp, scale=-1.0)
+            nc.scalar.activation(out=f2_raw[:], in_=lead_turned[:], func=FUNC.Exp)
+            return e1_raw, e2_raw, f1_raw, f2_raw
 
         def upright(turned_tile, name):
             bank = banks.tile([P, BLOCKS, P], F32, name=name)
@@ -260,45 +266,27 @@ def tile_rwkv_attention_pa_kernel(
                 nc.tensor.transpose(bank[:, b, :], turned_tile[:, b * P : (b + 1) * P], ident_f32[:])
             return bank
 
-        def project_v(i):
-            v_ps = banks.tile([P, BLOCKS, P], F32)
-            for b in range(BLOCKS):
-                rows = rows_of(i, b, 1)
-                for g in range(PASSES):
-                    nc.tensor.matmul_mx(
-                        out=v_ps[:, b, :],
-                        lhsT=xv_codes[:, g, rows].bitcast(FP8X4),
-                        lhsT_scale=xv_scales[:, g, rows],
-                        rhs=wv_codes[:, g, cols_of(i)].bitcast(FP8X4),
-                        rhs_scale=wv_scales[:, g, cols_of(i)],
-                        start=(g == 0),
-                        stop=(g == PASSES - 1),
-                    )
-            v_rows = work.tile([P, BLOCKS, P], F32)
-            nc.scalar.copy(out=v_rows[:], in_=v_ps[:])
-            return v_rows
-
         def clamped(out, raw, other, op):
             nc.vector.scalar_tensor_tensor(
                 out=out, in0=raw[:], scalar=1.0, in1=other, op0=ALU.min, op1=op
             )
 
         def blend(i, factor_banks, v_rows, aa, bb, num, den):
-            f1_ps, f2_ps, e1_ps, e2_ps = factor_banks
+            e1_ps, e2_ps, f1_ps, f2_ps = factor_banks
             a_part = a_rows[:, blocks_of(i), cols_of(i)]
             b_part = b_rows[:, blocks_of(i), cols_of(i)]
-            f2_v = work.tile([P, BLOCKS, P], F32)
             e2_v = work.tile([P, BLOCKS, P], F32)
-            clamped(aa, f1_ps, a_part, ALU.mult)
-            clamped(bb, f1_ps, b_part, ALU.mult)
-            clamped(f2_v[:], f2_ps, v_rows[:], ALU.mult)
-            clamped(bb, f2_ps, bb, ALU.add)
-            nc.gpsimd.tensor_tensor(out=aa, in0=aa, in1=f2_v[:], op=ALU.add)
+            f2_v = work.tile([P, BLOCKS, P], F32)
             clamped(num, e1_ps, a_part, ALU.mult)
             clamped(den, e1_ps, b_part, ALU.mult)
             clamped(e2_v[:], e2_ps, v_rows[:], ALU.mult)
             clamped(den, e2_ps, den, ALU.add)
             nc.gpsimd.tensor_tensor(out=num, in0=num, in1=e2_v[:], op=ALU.add)
+            clamped(aa, f1_ps, a_part, ALU.mult)
+            clamped(bb, f1_ps, b_part, ALU.mult)
+            clamped(f2_v[:], f2_ps, v_rows[:], ALU.mult)
+            clamped(bb, f2_ps, bb, ALU.add)
+            nc.gpsimd.tensor_tensor(out=aa, in0=aa, in1=f2_v[:], op=ALU.add)
 
         def store(out, group_tile, q):
             first_tile = q * GROUP
@@ -309,27 +297,20 @@ def tile_rwkv_attention_pa_kernel(
                 in_=group_tile[:].rearrange("p b n c -> p b (n c)"),
             )
 
-        turned_in = {0: turn(0)}
+        upright_in = {0: project(0)}
         raw = {}
-        v_in = {}
         factor_in = {}
         grouped_out = {}
-        for s in range(-2, TILES + 1):
+        for s in range(-2, TILES + GROUP):
             if s + 2 < TILES:
                 i = s + 2
                 if i % GROUP == 0:
                     p2_group = work.tile([P, BLOCKS, GROUP, P], F32)
-                p2_turned, raw[i] = gap(i, turned_in[i][0], turned_in[i][1])
-            if 0 <= s + 1 < TILES:
-                v_in[s + 1] = project_v(s + 1)
-            if s + 3 < TILES:
-                turned_in[s + 3] = turn(s + 3)
-            if s + 2 < TILES:
-                i = s + 2
-                p2_ps = upright(p2_turned, "p2_ps")
-                nc.scalar.copy(out=p2_group[:, :, i % GROUP, :], in_=p2_ps[:])
+                raw[i] = compare(i, upright_in[i][0], p2_group[:, :, i % GROUP, :])
                 if i % GROUP == GROUP - 1:
                     store(out_3, p2_group, i // GROUP)
+            if s + 3 < TILES:
+                upright_in[s + 3] = project(s + 3)
             if 0 <= s < TILES:
                 n = s % GROUP
                 if n == 0:
@@ -341,7 +322,7 @@ def tile_rwkv_attention_pa_kernel(
                 blend(
                     s,
                     factor_in[s],
-                    v_in[s],
+                    upright_in[s][1],
                     aa_group[:, :, n, :],
                     bb_group[:, :, n, :],
                     num_group[:, :, n, :],
@@ -354,9 +335,18 @@ def tile_rwkv_attention_pa_kernel(
                 factor_in[s + 1] = [
                     upright(raw[s + 1][n], name) for n, name in enumerate(FACTOR_BANKS)
                 ]
-            if s >= GROUP and s % GROUP == 0:
-                num_done, den_done = grouped_out[s // GROUP - 1]
-                nc.scalar.activation(out=den_done[:], in_=den_done[:], func=FUNC.Ln)
-                nc.scalar.activation(out=den_done[:], in_=den_done[:], func=FUNC.Exp, scale=-1.0)
-                nc.gpsimd.tensor_tensor(out=num_done[:], in0=num_done[:], in1=den_done[:], op=ALU.mult)
-                store(out_0, num_done, s // GROUP - 1)
+            if s >= GROUP:
+                q = s // GROUP - 1
+                b = s % GROUP
+                num_done, den_done = grouped_out[q]
+                if b == 0:
+                    nc.scalar.activation(out=den_done[:], in_=den_done[:], func=FUNC.Ln)
+                nc.scalar.activation(out=den_done[:, b], in_=den_done[:, b], func=FUNC.Exp, scale=-1.0)
+                wkv_rows = work.tile([P, GROUP, P], F32, bufs=3)
+                nc.gpsimd.tensor_tensor(
+                    out=wkv_rows[:], in0=num_done[:, b], in1=den_done[:, b], op=ALU.mult
+                )
+                nc.sync.dma_start(
+                    out=out_0[rows_of(q * GROUP, b, 1), cols_of(q * GROUP, GROUP)],
+                    in_=wkv_rows[:].rearrange("p n c -> p (n c)"),
+                )

@@ -132,9 +132,10 @@ def tile_rwkv_attention_pa_kernel(
             make_identity(nc, ident[:])
             make_identity(nc, ident_f32[:])
             for r in range(ROW_TILES):
-                nc.gpsimd.tensor_tensor(
-                    out=decayed[:, r, :], in0=p_rows[:, r, :], in1=decay_rows[:], op=ALU.add
-                )
+                for cols in (slice(0, N_TILE), slice(N_TILE, WIDTH)):
+                    nc.gpsimd.tensor_tensor(
+                        out=decayed[:, r, cols], in0=p_rows[:, r, cols], in1=decay_rows[:, cols], op=ALU.add
+                    )
             vectors_turned = turned.tile([P, P], BF16, tag="x_turned")
             nc.tensor.transpose(vectors_turned[:], vector_rows[:], ident[:])
             nc.vector.tensor_copy(out=columns[:], in_=vectors_turned[:, 0 : 4 * CHUNKS])
@@ -343,7 +344,8 @@ def tile_rwkv_attention_pa_kernel(
                     nc.scalar.activation(out=den_done[:], in_=den_done[:], func=FUNC.Ln)
                 nc.scalar.activation(out=den_done[:, b], in_=den_done[:, b], func=FUNC.Exp, scale=-1.0)
                 wkv_rows = work.tile([P, GROUP, P], F32, bufs=3)
-                nc.gpsimd.tensor_tensor(
+                multiplier = nc.vector if q == TILES // GROUP - 1 else nc.gpsimd
+                multiplier.tensor_tensor(
                     out=wkv_rows[:], in0=num_done[:, b], in1=den_done[:, b], op=ALU.mult
                 )
                 nc.sync.dma_start(

@@ -84,7 +84,7 @@ def tile_rwkv_attention_pa_kernel(
         xv_scales = keep.tile([P, PASSES, ROWS], U8, align_bytes=64)
         wk_scales = keep.tile([P, PASSES, WIDTH], U8, align_bytes=64)
         wv_scales = keep.tile([P, PASSES, WIDTH], U8, align_bytes=64)
-        decayed = keep.tile([P, ROW_TILES, WIDTH], F32)
+        p_rows = keep.tile([P, ROW_TILES, WIDTH], BF16)
         decay_rows = keep.tile([P, WIDTH], BF16)
         ident = keep.tile([P, P], BF16)
         ident_f32 = keep.tile([P, P], F32)
@@ -113,7 +113,6 @@ def tile_rwkv_attention_pa_kernel(
             s_rows = whole.tile([P, ROW_TILES, DEPTH], BF16)
             wk_planes = whole.tile([P, PASSES, PACK, WIDTH], BF16)
             wv_planes = whole.tile([P, PASSES, PACK, WIDTH], BF16)
-            p_rows = whole.tile([P, ROW_TILES, WIDTH], BF16)
             x_view = x.rearrange("(r p) d -> p r d", p=P)
             s_view = saved_x.rearrange("(r p) d -> p r d", p=P)
             wk_view = key_weight.rearrange("(g t p) a -> g p t a", t=PACK, p=P)
@@ -131,11 +130,6 @@ def tile_rwkv_attention_pa_kernel(
 
             make_identity(nc, ident[:])
             make_identity(nc, ident_f32[:])
-            for r in range(ROW_TILES):
-                for cols in (slice(0, N_TILE), slice(N_TILE, WIDTH)):
-                    nc.gpsimd.tensor_tensor(
-                        out=decayed[:, r, cols], in0=p_rows[:, r, cols], in1=decay_rows[:, cols], op=ALU.add
-                    )
             vectors_turned = turned.tile([P, P], BF16, tag="x_turned")
             nc.tensor.transpose(vectors_turned[:], vector_rows[:], ident[:])
             nc.vector.tensor_copy(out=columns[:], in_=vectors_turned[:, 0 : 4 * CHUNKS])
@@ -236,14 +230,20 @@ def tile_rwkv_attention_pa_kernel(
                         )
             v_rows = work.tile([P, BLOCKS, P], F32, bufs=4)
             nc.scalar.copy(out=v_rows[:], in_=v_ps[:])
-            return k_ps, v_rows
+            decayed = work.tile([P, BLOCKS, P], F32, bufs=3)
+            nc.gpsimd.tensor_tensor(
+                out=decayed[:],
+                in0=p_rows[:, blocks_of(i), cols_of(i)],
+                in1=decay_rows[:, cols_of(i)].unsqueeze(1).to_broadcast([P, BLOCKS, P]),
+                op=ALU.add,
+            )
+            return k_ps, v_rows, decayed
 
-        def compare(i, k_ps, p2):
+        def compare(i, k_ps, decayed, p2):
             j = i % COL_BLOCKS
-            decayed_part = decayed[:, blocks_of(i), cols_of(i)]
             lead = work.tile([P, BLOCKS, P], F32)
-            nc.vector.tensor_tensor(out=lead[:], in0=k_ps[:], in1=decayed_part, op=ALU.subtract)
-            nc.vector.tensor_tensor(out=p2, in0=k_ps[:], in1=decayed_part, op=ALU.max)
+            nc.vector.tensor_tensor(out=lead[:], in0=k_ps[:], in1=decayed[:], op=ALU.subtract)
+            nc.vector.tensor_tensor(out=p2, in0=k_ps[:], in1=decayed[:], op=ALU.max)
             lead_turned = early.tile([P, N_TILE], F32)
             for b in range(BLOCKS):
                 nc.tensor.transpose(lead_turned[:, b * P : (b + 1) * P], lead[:, b, :], ident_f32[:])
@@ -307,7 +307,7 @@ def tile_rwkv_attention_pa_kernel(
                 i = s + 2
                 if i % GROUP == 0:
                     p2_group = work.tile([P, BLOCKS, GROUP, P], F32)
-                raw[i] = compare(i, upright_in[i][0], p2_group[:, :, i % GROUP, :])
+                raw[i] = compare(i, upright_in[i][0], upright_in[i][2], p2_group[:, :, i % GROUP, :])
                 if i % GROUP == GROUP - 1:
                     store(out_3, p2_group, i // GROUP)
             if s + 3 < TILES:
@@ -344,8 +344,7 @@ def tile_rwkv_attention_pa_kernel(
                     nc.scalar.activation(out=den_done[:], in_=den_done[:], func=FUNC.Ln)
                 nc.scalar.activation(out=den_done[:, b], in_=den_done[:, b], func=FUNC.Exp, scale=-1.0)
                 wkv_rows = work.tile([P, GROUP, P], F32, bufs=3)
-                multiplier = nc.vector if q == TILES // GROUP - 1 else nc.gpsimd
-                multiplier.tensor_tensor(
+                nc.gpsimd.tensor_tensor(
                     out=wkv_rows[:], in0=num_done[:, b], in1=den_done[:, b], op=ALU.mult
                 )
                 nc.sync.dma_start(

from contextlib import ExitStack

import concourse.mybir as mybir
from concourse.masks import make_identity

F32 = mybir.dt.float32
BF16 = mybir.dt.bfloat16
U32 = mybir.dt.uint32
U8 = mybir.dt.uint8
FP8X4 = mybir.dt.float8_e4m3fn_x4
ALU = mybir.AluOpType
FUNC = mybir.ActivationFunctionType

P = 128
PACK = 4
K_PASS = P * PACK
ROWS = 1024
DEPTH = 1024
WIDTH = 1024
PASSES = DEPTH // K_PASS
CHUNKS = DEPTH // P
ROW_TILES = ROWS // P
N_TILE = 512
ROW_HALVES = ROWS // N_TILE
BLOCKS = N_TILE // P
COL_BLOCKS = WIDTH // P
TILES = ROW_HALVES * COL_BLOCKS
FACTOR_BANKS = ("e1_ps", "e2_ps", "f1_ps", "f2_ps")
GROUP = 4
VECTOR_SHARE = 640
assert BLOCKS == GROUP

FLOPS = 2 * 2 * ROWS * DEPTH * WIDTH


def interleave(nc, grouped, planes):
    nc.vector.tensor_copy(
        out=grouped[:, 0:VECTOR_SHARE, :].rearrange("p (c i) t -> p c t i", i=4),
        in_=planes[:, :, 0:VECTOR_SHARE].rearrange("p t (c i) -> p c t i", i=4),
    )
    nc.scalar.copy(
        out=grouped[:, VECTOR_SHARE:, :].rearrange("p (c i) t -> p c t i", i=4),
        in_=planes[:, :, VECTOR_SHARE:].rearrange("p t (c i) -> p c t i", i=4),
    )


def quantise(nc, grouped, codes, scales):
    nc.vector.quantize_mx(
        out=codes.bitcast(FP8X4),
        scales=scales,
        in_=grouped.rearrange("p c t -> p (c t)"),
    )


def tile_rwkv_attention_pa_kernel(
    tc,
    x,
    saved_x,
    saved_a,
    saved_b,
    saved_p,
    time_decay,
    time_first,
    k_mixed,
    v_mixed,
    key_weight,
    value_weight,
    out_0,
    out_1,
    out_2,
    out_3,
):
    nc = tc.nc
    with ExitStack() as pools:
        pools.enter_context(tc.manual_schedule())
        keep = pools.enter_context(tc.tile_pool(name="keep", bufs=1))
        early = pools.enter_context(tc.psum_pool(name="early", bufs=1))

        xk_codes = keep.tile([P, PASSES, ROWS], U32, align_bytes=64)
        xv_codes = keep.tile([P, PASSES, ROWS], U32, align_bytes=64)
        wk_codes = keep.tile([P, PASSES, WIDTH], U32, align_bytes=64)
        wv_codes = keep.tile([P, PASSES, WIDTH], U32, align_bytes=64)
        xk_scales = keep.tile([P, PASSES, ROWS], U8, align_bytes=64)
        xv_scales = keep.tile([P, PASSES, ROWS], U8, align_bytes=64)
        wk_scales = keep.tile([P, PASSES, WIDTH], U8, align_bytes=64)
        wv_scales = keep.tile([P, PASSES, WIDTH], U8, align_bytes=64)
        p_rows = keep.tile([P, ROW_TILES, WIDTH], BF16)
        decay_rows = keep.tile([P, WIDTH], BF16)
        ident = keep.tile([P, P], BF16)
        ident_f32 = keep.tile([P, P], F32)
        vector_rows = keep.tile([P, P], BF16)
        columns = keep.tile([P, 4 * CHUNKS], F32)
        one_minus_mix = keep.tile([P, 2 * CHUNKS], F32)
        shift = keep.tile([P, CHUNKS], F32)
        minus_shift = keep.tile([P, CHUNKS], F32)
        mix = columns[:, 0 : 2 * CHUNKS]
        decay = columns[:, 2 * CHUNKS : 3 * CHUNKS]
        first = columns[:, 3 * CHUNKS : 4 * CHUNKS]

        with ExitStack() as operand_pools:
            whole = operand_pools.enter_context(tc.tile_pool(name="whole", bufs=1))
            stage = operand_pools.enter_context(tc.tile_pool(name="stage", bufs=2))
            group = operand_pools.enter_context(tc.tile_pool(name="group", bufs=4))
            turned = operand_pools.enter_context(tc.psum_pool(name="turned", bufs=2))

            nc.vector.memset(vector_rows[:], 0.0)
            for n, vector in enumerate((k_mixed, v_mixed, time_decay, time_first)):
                nc.sync.dma_start(
                    out=vector_rows[n * CHUNKS : (n + 1) * CHUNKS, :],
                    in_=vector.rearrange("(c p) -> c p", p=P),
                )
            x_rows = whole.tile([P, ROW_TILES, DEPTH], BF16)
            s_rows = whole.tile([P, ROW_TILES, DEPTH], BF16)
            wk_planes = whole.tile([P, PASSES, PACK, WIDTH], BF16)
            wv_planes = whole.tile([P, PASSES, PACK, WIDTH], BF16)
            x_view = x.rearrange("(r p) d -> p r d", p=P)
            s_view = saved_x.rearrange("(r p) d -> p r d", p=P)
            wk_view = key_weight.rearrange("(g t p) a -> g p t a", t=PACK, p=P)
            wv_view = value_weight.rearrange("(g t p) a -> g p t a", t=PACK, p=P)
            nc.sync.dma_start(out=wk_planes[:, 0], in_=wk_view[0])
            nc.sync.dma_start(out=wv_planes[:, 0], in_=wv_view[0])
            for g in range(PASSES):
                depth = slice(g * K_PASS, (g + 1) * K_PASS)
                nc.sync.dma_start(out=s_rows[:, :, depth], in_=s_view[:, :, depth])
                nc.sync.dma_start(out=x_rows[:, :, depth], in_=x_view[:, :, depth])
            nc.sync.dma_start(out=wk_planes[:, 1], in_=wk_view[1])
            nc.sync.dma_start(out=wv_planes[:, 1], in_=wv_view[1])
            nc.sync.dma_start(out=decay_rows[:], in_=time_decay.partition_broadcast(P))
            nc.sync.dma_start(out=p_rows[:], in_=saved_p.rearrange("(r p) a -> p r a", p=P))

            make_identity(nc, ident[:])
            make_identity(nc, ident_f32[:])
            vectors_turned = turned.tile([P, P], BF16, tag="x_turned")
            nc.tensor.transpose(vectors_turned[:], vector_rows[:], ident[:])
            nc.vector.tensor_copy(out=columns[:], in_=vectors_turned[:, 0 : 4 * CHUNKS])
            nc.vector.tensor_scalar(
                out=one_minus_mix[:], in0=mix, scalar1=-1.0, scalar2=1.0, op0=ALU.mult, op1=ALU.add
            )
            nc.vector.tensor_tensor(out=shift[:], in0=decay, in1=first, op=ALU.add)
            nc.vector.tensor_scalar_mul(out=minus_shift[:], in0=shift[:], scalar1=-1.0)

            def quantise_pair(g, k_source, v_source, k_codes, k_scales, v_codes, v_scales):
                k_grouped = group.tile([P, WIDTH, PACK], BF16, tag="grouped", align_bytes=64)
                v_grouped = group.tile([P, WIDTH, PACK], BF16, tag="grouped", align_bytes=64)
                interleave(nc, k_grouped[:], k_source)
                interleave(nc, v_grouped[:], v_source)
                quantise(nc, k_grouped[:], k_codes[:, g, :], k_scales[:, g, :])
                quantise(nc, v_grouped[:], v_codes[:, g, :], v_scales[:, g, :])

            def mix_pass(g):
                k_planes = stage.tile([P, PACK, ROWS], BF16)
                v_planes = stage.tile([P, PACK, ROWS], BF16)
                for t in range(PACK):
                    c = g * PACK + t
                    s_turned = turned.tile([P, ROWS], BF16)
                    x_turned = turned.tile([P, ROWS], BF16)
                    for r in range(ROW_TILES):
                        nc.tensor.transpose(
                            s_turned[:, r * P : (r + 1) * P], s_rows[:, r, c * P : (c + 1) * P], ident[:]
                        )
                    for r in range(ROW_TILES):
                        nc.tensor.transpose(
                            x_turned[:, r * P : (r + 1) * P], x_rows[:, r, c * P : (c + 1) * P], ident[:]
                        )
                    for planes, col in ((k_planes, c), (v_planes, CHUNKS + c)):
                        old_part = stage.tile([P, ROWS], F32)
                        nc.scalar.activation(
                            out=old_part[:],
                            in_=s_turned[:],
                            func=FUNC.Copy,
                            scale=one_minus_mix[:, col : col + 1],
                        )
                        nc.vector.scalar_tensor_tensor(
                            out=planes[:, t, :],
                            in0=x_turned[:],
                            scalar=mix[:, col : col + 1],
                            in1=old_part[:],
                            op0=ALU.mult,
                            op1=ALU.add,
                        )
                return k_planes, v_planes

            for g in range(PASSES):
                quantise_pair(
                    g, wk_planes[:, g], wv_planes[:, g], wk_codes, wk_scales, wv_codes, wv_scales
                )
                k_planes, v_planes = mix_pass(g)
                quantise_pair(g, k_planes[:], v_planes[:], xk_codes, xk_scales, xv_codes, xv_scales)

        late = pools.enter_context(tc.tile_pool(name="late", bufs=1, reuse_waits="tile"))
        work = pools.enter_context(tc.tile_pool(name="work", bufs=2, reuse_waits="tile"))
        banks = pools.enter_context(tc.psum_pool(name="banks", bufs=1, reuse_waits="tile"))
        a_rows = late.tile([P, ROW_TILES, WIDTH], BF16)
        b_rows = late.tile([P, ROW_TILES, WIDTH], BF16)
        for h in range(ROW_HALVES):
            blocks = slice(h * BLOCKS, (h + 1) * BLOCKS)
            for rows_tile, source in ((a_rows, saved_a), (b_rows, saved_b)):
                nc.sync.dma_start(
                    out=rows_tile[:, blocks, :],
                    in_=source.rearrange("(r p) a -> p r a", p=P)[:, blocks, :],
                )

        def rows_of(i, b=0, count=BLOCKS):
            first_row = (i // COL_BLOCKS) * N_TILE + b * P
            return slice(first_row, first_row + count * P)

        def blocks_of(i):
            return slice((i // COL_BLOCKS) * BLOCKS, (i // COL_BLOCKS + 1) * BLOCKS)

        def cols_of(i, count=1):
            return slice((i % COL_BLOCKS) * P, (i % COL_BLOCKS + count) * P)

        def project(i):
            k_ps = early.tile([P, BLOCKS, P], F32)
            v_ps = early.tile([P, BLOCKS, P], F32)
            for acc, x_codes, x_scales, w_codes, w_scales in (
                (k_ps, xk_codes, xk_scales, wk_codes, wk_scales),
                (v_ps, xv_codes, xv_scales, wv_codes, wv_scales),
            ):
                for b in range(BLOCKS):
                    for g in range(PASSES):
                        nc.tensor.matmul_mx(
                            out=acc[:, b, :],
                            lhsT=x_codes[:, g, rows_of(i, b, 1)].bitcast(FP8X4),
                            lhsT_scale=x_scales[:, g, rows_of(i, b, 1)],
                            rhs=w_codes[:, g, cols_of(i)].bitcast(FP8X4),
                            rhs_scale=w_scales[:, g, cols_of(i)],
                            start=(g == 0),
                            stop=(g == PASSES - 1),
                        )
            v_rows = work.tile([P, BLOCKS, P], F32, bufs=4)
            nc.scalar.copy(out=v_rows[:], in_=v_ps[:])
            decayed = work.tile([P, BLOCKS, P], F32, bufs=3)
            nc.gpsimd.tensor_tensor(
                out=decayed[:],
                in0=p_rows[:, blocks_of(i), cols_of(i)],
                in1=decay_rows[:, cols_of(i)].unsqueeze(1).to_broadcast([P, BLOCKS, P]),
                op=ALU.add,
            )
            return k_ps, v_rows, decayed

        def compare(i, k_ps, decayed, p2):
            j = i % COL_BLOCKS
            lead = work.tile([P, BLOCKS, P], F32)
            nc.vector.tensor_tensor(out=lead[:], in0=k_ps[:], in1=decayed[:], op=ALU.subtract)
            nc.vector.tensor_tensor(out=p2, in0=k_ps[:], in1=decayed[:], op=ALU.max)
            lead_turned = early.tile([P, N_TILE], F32)
            for b in range(BLOCKS):
                nc.tensor.transpose(lead_turned[:, b * P : (b + 1) * P], lead[:, b, :], ident_f32[:])
            e1_raw = work.tile([P, N_TILE], F32)
            e2_raw = work.tile([P, N_TILE], F32)
            f1_raw = work.tile([P, N_TILE], F32)
            f2_raw = work.tile([P, N_TILE], F32)
            nc.scalar.activation(
                out=e1_raw[:], in_=lead_turned[:], func=FUNC.Exp, scale=-1.0, bias=minus_shift[:, j : j + 1]
            )
            nc.scalar.activation(
                out=e2_raw[:], in_=lead_turned[:], func=FUNC.Exp, bias=shift[:, j : j + 1]
            )
            nc.scalar.activation(out=f1_raw[:], in_=lead_turned[:], func=FUNC.Exp, scale=-1.0)
            nc.scalar.activation(out=f2_raw[:], in_=lead_turned[:], func=FUNC.Exp)
            return e1_raw, e2_raw, f1_raw, f2_raw

        def upright(turned_tile, name):
            bank = banks.tile([P, BLOCKS, P], F32, name=name)
            for b in range(BLOCKS):
                nc.tensor.transpose(bank[:, b, :], turned_tile[:, b * P : (b + 1) * P], ident_f32[:])
            return bank

        def clamped(out, raw, other, op):
            nc.vector.scalar_tensor_tensor(
                out=out, in0=raw[:], scalar=1.0, in1=other, op0=ALU.min, op1=op
            )

        def blend(i, factor_banks, v_rows, aa, bb, num, den):
            e1_ps, e2_ps, f1_ps, f2_ps = factor_banks
            a_part = a_rows[:, blocks_of(i), cols_of(i)]
            b_part = b_rows[:, blocks_of(i), cols_of(i)]
            e2_v = work.tile([P, BLOCKS, P], F32)
            f2_v = work.tile([P, BLOCKS, P], F32)
            clamped(num, e1_ps, a_part, ALU.mult)
            clamped(den, e1_ps, b_part, ALU.mult)
            clamped(e2_v[:], e2_ps, v_rows[:], ALU.mult)
            clamped(den, e2_ps, den, ALU.add)
            nc.gpsimd.tensor_tensor(out=num, in0=num, in1=e2_v[:], op=ALU.add)
            clamped(aa, f1_ps, a_part, ALU.mult)
            clamped(bb, f1_ps, b_part, ALU.mult)
            clamped(f2_v[:], f2_ps, v_rows[:], ALU.mult)
            clamped(bb, f2_ps, bb, ALU.add)
            nc.gpsimd.tensor_tensor(out=aa, in0=aa, in1=f2_v[:], op=ALU.add)

        def store(out, group_tile, q):
            first_tile = q * GROUP
            nc.sync.dma_start(
                out=out.rearrange("(r p) a -> p r a", p=P)[
                    :, blocks_of(first_tile), cols_of(first_tile, GROUP)
                ],
                in_=group_tile[:].rearrange("p b n c -> p b (n c)"),
            )

        upright_in = {0: project(0)}
        raw = {}
        factor_in = {}
        grouped_out = {}
        for s in range(-2, TILES + GROUP):
            if s + 2 < TILES:
                i = s + 2
                if i % GROUP == 0:
                    p2_group = work.tile([P, BLOCKS, GROUP, P], F32)
                raw[i] = compare(i, upright_in[i][0], upright_in[i][2], p2_group[:, :, i % GROUP, :])
                if i % GROUP == GROUP - 1:
                    store(out_3, p2_group, i // GROUP)
            if s + 3 < TILES:
                upright_in[s + 3] = project(s + 3)
            if 0 <= s < TILES:
                n = s % GROUP
                if n == 0:
                    aa_group = work.tile([P, BLOCKS, GROUP, P], F32)
                    bb_group = work.tile([P, BLOCKS, GROUP, P], F32)
                    num_group = work.tile([P, BLOCKS, GROUP, P], F32)
                    den_group = work.tile([P, BLOCKS, GROUP, P], F32)
                    grouped_out[s // GROUP] = (num_group, den_group)
                blend(
                    s,
                    factor_in[s],
                    upright_in[s][1],
                    aa_group[:, :, n, :],
                    bb_group[:, :, n, :],
                    num_group[:, :, n, :],
                    den_group[:, :, n, :],
                )
                if n == GROUP - 1:
                    store(out_1, aa_group, s // GROUP)
                    store(out_2, bb_group, s // GROUP)
            if 0 <= s + 1 < TILES:
                factor_in[s + 1] = [
                    upright(raw[s + 1][n], name) for n, name in enumerate(FACTOR_BANKS)
                ]
            if s >= GROUP:
                q = s // GROUP - 1
                b = s % GROUP
                num_done, den_done = grouped_out[q]
                if b == 0:
                    nc.scalar.activation(out=den_done[:], in_=den_done[:], func=FUNC.Ln)
                nc.scalar.activation(out=den_done[:, b], in_=den_done[:, b], func=FUNC.Exp, scale=-1.0)
                wkv_rows = work.tile([P, GROUP, P], F32, bufs=3)
                nc.gpsimd.tensor_tensor(
                    out=wkv_rows[:], in0=num_done[:, b], in1=den_done[:, b], op=ALU.mult
                )
                nc.sync.dma_start(
                    out=out_0[rows_of(q * GROUP, b, 1), cols_of(q * GROUP, GROUP)],
                    in_=wkv_rows[:].rearrange("p n c -> p (n c)"),
                )
